import numpy as np
import ml_dtypes


def mxq(x, axis, fmt="e4m3"):
    dtype, down = {"e4m3": (ml_dtypes.float8_e4m3fn, 7), "e5m2": (ml_dtypes.float8_e5m2, 14)}[fmt]
    v = np.moveaxis(np.asarray(x, np.float32).astype(ml_dtypes.bfloat16).astype(np.float64), axis, -1)
    blocks = v.reshape(v.shape[:-1] + (-1, 32))
    amax = np.abs(blocks).max(-1, keepdims=True)
    byte = np.maximum(np.where(amax > 0, np.frexp(amax)[1] - 1 + 127, 0) - down, 1)
    scale = np.exp2(byte - 127.0)
    codes = (blocks / scale).astype(np.float32).astype(dtype).astype(np.float64)
    return np.moveaxis((codes * scale).reshape(v.shape), -1, axis)


WIDE = False


def mx_kscale(k):
    if not WIDE:
        return np.ones(k)
    levels = np.array([10, -10, 5, -5, 0])
    if k % 512:
        return np.exp2(np.random.permutation(np.resize(levels, k // 32))).repeat(32)
    a = np.empty((k // 512, 16))
    for p in range(k // 512):
        a[p, :8] = np.random.permutation(np.resize(levels, 8))
        for g in range(8):
            far = levels[np.abs(levels - a[p, g]) >= 10]
            a[p, g + 8] = far[np.random.randint(len(far))]
    return np.exp2(a.ravel()).repeat(32)


BF16 = ml_dtypes.bfloat16


def bf(x):
    return np.asarray(x, np.float32).astype(BF16)


def f64(x):
    return np.asarray(x).astype(np.float64)


SL, BS, DM, H, NH, DO = 32, 128, 1024, 16, 64, 1024
DP = H * NH


def setup_inputs():
    s, t = mx_kscale(DM), mx_kscale(DP)
    g = np.random.standard_normal((SL, BS, H)) * 2.0
    return {"values": bf(np.random.standard_normal((SL, BS, DM)) * s),
            "logw": bf(g - np.log(np.exp(g).sum(0, keepdims=True))),
            "Wv": bf(np.random.standard_normal((DP, DM)) / np.sqrt(DM * SL) / s * t[:, None]),
            "Wo": bf(np.random.standard_normal((DO, DP)) * 0.5 / np.sqrt(DP) / t)}


def reference(values, logw, Wv, Wo):
    vp = mxq(f64(values), 2, "e4m3") @ mxq(f64(Wv), 1, "e4m3").T
    attn = (f64(logw)[..., None] * vp.reshape(SL, BS, H, NH)).sum(0)
    return mxq(attn.reshape(BS, DP), 1, "e4m3") @ mxq(f64(Wo), 1, "e4m3").T

@@ -1,0 +1,234 @@
+from contextlib import ExitStack
+
+import concourse.mybir as mybir
+from concourse.masks import make_identity
+
+F32 = mybir.dt.float32
+BF16 = mybir.dt.bfloat16
+U32 = mybir.dt.uint32
+U8 = mybir.dt.uint8
+FP8X4 = mybir.dt.float8_e4m3fn_x4
+MULT = mybir.AluOpType.mult
+ADD = mybir.AluOpType.add
+COPY = mybir.ActivationFunctionType.Copy
+
+P = 128
+SL, DM, HEADS, HEAD_DIM, DO = 32, 1024, 16, 64, 1024
+DP = HEADS * HEAD_DIM
+K_PASS = 512
+PASSES = DM // K_PASS
+N_TILE = 512
+HALVES = DP // N_TILE
+HEADS_PER_HALF = N_TILE // HEAD_DIM
+GROUP = 4
+N_GROUPS = SL // GROUP
+W_UNITS = DP // P
+UNIT_WORDS = PASSES * P
+
+FLOPS = 2 * SL * P * DM * DP + 2 * P * DP * DO
+
+
+def tile_multiheadattention_pb_kernel(tc, values, logw, Wv, Wo, out):
+    nc = tc.nc
+    with ExitStack() as ctx:
+        keep = ctx.enter_context(tc.tile_pool(name="keep", bufs=1))
+        stage = ctx.enter_context(tc.tile_pool(name="stage", bufs=2))
+        sums_psum = ctx.enter_context(tc.psum_pool(name="sums", bufs=4))
+        ctx.enter_context(tc.manual_schedule())
+
+        ident = keep.tile([P, P], F32)
+        make_identity(nc, ident[:])
+        acc = keep.tile([P, DP], F32)
+        nc.vector.memset(acc[:], 0.0)
+        acc_side = keep.tile([P, DP], F32)
+        nc.gpsimd.memset(acc_side[:], 0.0)
+
+        x_raw = [keep.tile([P, GROUP * DM], BF16, name="x_raw%d" % i) for i in range(N_GROUPS)]
+        wv_raw = keep.tile([P, W_UNITS * DM], BF16)
+        wo_raw = keep.tile([P, W_UNITS * DM], BF16)
+        lw_bf = keep.tile([P, SL, HEADS], BF16)
+        lw = keep.tile([P, SL, HEADS], F32)
+        val_codes = keep.tile([P, SL * UNIT_WORDS], U32, align_bytes=64)
+        val_scales = keep.tile([P, SL * UNIT_WORDS], U8, align_bytes=64)
+        wv_codes = keep.tile([P, PASSES * DP], U32, align_bytes=64)
+        wv_scales = keep.tile([P, PASSES * DP], U8, align_bytes=64)
+        wo_codes = keep.tile([P, PASSES * DO], U32, align_bytes=64)
+        wo_scales = keep.tile([P, PASSES * DO], U8, align_bytes=64)
+        attn_grouped = keep.tile([P, 4 * UNIT_WORDS], BF16, align_bytes=64)
+        attn_codes = keep.tile([P, UNIT_WORDS], U32, align_bytes=64)
+        attn_scales = keep.tile([P, UNIT_WORDS], U8, align_bytes=64)
+        out_sb = keep.tile([P, DO], F32)
+
+        def load_two_units(raw, slot, matrix, unit):
+            src = matrix[unit * P : (unit + 2) * P, :].rearrange("(t p) k -> p t k", p=P)
+            dst = raw[:, slot * DM : (slot + 2) * DM].rearrange("p (t k) -> p t k", t=2)
+            nc.sync.dma_start(out=dst, in_=src)
+
+        value_rows = values.flatten_outer_dims()
+
+        def load_group(i):
+            positions = slice(GROUP * i, GROUP * (i + 1))
+            nc.sync.dma_start(
+                out=lw_bf[:, positions, :], in_=logw[positions].rearrange("s b h -> b s h")
+            )
+            for t in range(0, GROUP, 2):
+                load_two_units(x_raw[i], t, value_rows, GROUP * i + t)
+
+        for u in range(0, W_UNITS // 2, 2):
+            load_two_units(wv_raw, u, Wv, u)
+        load_group(0)
+        for u in range(W_UNITS // 2, W_UNITS, 2):
+            load_two_units(wv_raw, u, Wv, u)
+        for i in range(1, N_GROUPS):
+            load_group(i)
+            if i % 2 == 1:
+                load_two_units(wo_raw, i - 1, Wo, i - 1)
+
+        def flip_unit(flip_psum, rows, grouped_words):
+            words = rows.bitcast(F32)
+            flipped = flip_psum.tile([P, PASSES, 2, P], F32, tag="flipped")
+            for g in range(PASSES):
+                for u in range(2):
+                    every_2nd = slice(2 * P * g + u, 2 * P * (g + 1), 2)
+                    nc.tensor.transpose(flipped[:, g, u, :], words[:, every_2nd], ident[:])
+            nc.scalar.copy(out=grouped_words, in_=flipped[:].rearrange("p g u r -> p g r u"))
+
+        def quantise(grouped, codes, scales):
+            nc.vector.quantize_mx(out=codes.bitcast(FP8X4), scales=scales, in_=grouped)
+
+        def flip_values(flip_psum, i):
+            grouped = stage.tile([P, GROUP * 4 * UNIT_WORDS], BF16, tag="x_grouped", align_bytes=64)
+            words = grouped[:].bitcast(F32).rearrange(
+                "p (t g r u) -> p t g r u", t=GROUP, g=PASSES, u=2
+            )
+            for t in range(GROUP):
+                flip_unit(flip_psum, x_raw[i][:, t * DM : (t + 1) * DM], words[:, t])
+            positions = slice(GROUP * i, GROUP * (i + 1))
+            nc.vector.tensor_copy(out=lw[:, positions, :], in_=lw_bf[:, positions, :])
+            return grouped
+
+        def quantise_values(grouped, i, pair):
+            n = 2 * UNIT_WORDS
+            first = (GROUP * i + 2 * pair) * UNIT_WORDS
+            quantise(
+                grouped[:, pair * 4 * n : (pair + 1) * 4 * n],
+                val_codes[:, first : first + n],
+                val_scales[:, first : first + n],
+            )
+
+        def flip_weight_unit(flip_psum, raw, unit):
+            grouped = stage.tile([P, 4 * UNIT_WORDS], BF16, tag="w_grouped", bufs=3, align_bytes=64)
+            words = grouped[:].bitcast(F32).rearrange("p (g r u) -> p g r u", g=PASSES, u=2)
+            flip_unit(flip_psum, raw[:, unit * DM : (unit + 1) * DM], words)
+            return grouped
+
+        def quantise_weight_unit(grouped, codes, scales, unit):
+            for g in range(PASSES):
+                first = g * DP + unit * P
+                quantise(
+                    grouped[:, g * 4 * P : (g + 1) * 4 * P],
+                    codes[:, first : first + P],
+                    scales[:, first : first + P],
+                )
+
+        def project_and_pool(s, half, on_the_side):
+            vp = sums_psum.tile([P, N_TILE], F32, tag="vp")
+            for g in range(PASSES):
+                rows = slice((s * PASSES + g) * P, (s * PASSES + g + 1) * P)
+                cols = slice(g * DP + half * N_TILE, g * DP + (half + 1) * N_TILE)
+                nc.tensor.matmul_mx(
+                    out=vp[:],
+                    lhsT=val_codes[:, rows].bitcast(FP8X4),
+                    lhsT_scale=val_scales[:, rows],
+                    rhs=wv_codes[:, cols].bitcast(FP8X4),
+                    rhs_scale=wv_scales[:, cols],
+                    start=(g == 0),
+                    stop=(g == PASSES - 1),
+                )
+            if on_the_side:
+                weighted = stage.tile([P, N_TILE], F32, tag="weighted")
+            for j in range(HEADS_PER_HALF):
+                h = half * HEADS_PER_HALF + j
+                channels = slice(h * HEAD_DIM, (h + 1) * HEAD_DIM)
+                bank_cols = slice(j * HEAD_DIM, (j + 1) * HEAD_DIM)
+                if on_the_side:
+                    nc.scalar.activation(
+                        out=weighted[:, bank_cols], in_=vp[:, bank_cols], func=COPY, scale=lw[:, s, h : h + 1]
+                    )
+                else:
+                    nc.vector.scalar_tensor_tensor(
+                        out=acc[:, channels],
+                        in0=vp[:, bank_cols],
+                        scalar=lw[:, s, h : h + 1],
+                        in1=acc[:, channels],
+                        op0=MULT,
+                        op1=ADD,
+                    )
+            if on_the_side:
+                side = acc_side[:, half * N_TILE : (half + 1) * N_TILE]
+                nc.gpsimd.tensor_tensor(out=side, in0=side, in1=weighted[:], op=ADD)
+
+        def join_sums(half):
+            cols = slice(half * N_TILE, (half + 1) * N_TILE)
+            nc.gpsimd.tensor_tensor(out=acc[:, cols], in0=acc[:, cols], in1=acc_side[:, cols], op=ADD)
+
+        with tc.psum_pool(name="flip", bufs=4) as flip_psum:
+            for unit in range(W_UNITS // 2):
+                w_grouped = flip_weight_unit(flip_psum, wv_raw, unit)
+                quantise_weight_unit(w_grouped, wv_codes, wv_scales, unit)
+            x_grouped = flip_values(flip_psum, 0)
+            quantise_values(x_grouped, 0, 0)
+            quantise_values(x_grouped, 0, 1)
+            for unit in range(W_UNITS // 2, W_UNITS):
+                w_grouped = flip_weight_unit(flip_psum, wv_raw, unit)
+                quantise_weight_unit(w_grouped, wv_codes, wv_scales, unit)
+
+            for i in range(N_GROUPS):
+                more_values = i + 1 < N_GROUPS
+                if not more_values:
+                    join_sums(1)
+                for t in range(GROUP):
+                    project_and_pool(GROUP * i + t, 0, t == 0)
+                if not more_values:
+                    join_sums(0)
+                if more_values:
+                    x_grouped = flip_values(flip_psum, i + 1)
+                w_grouped = flip_weight_unit(flip_psum, wo_raw, i)
+                for t in range(GROUP):
+                    if t < 2 and more_values:
+                        quantise_values(x_grouped, i + 1, t)
+                    if t == 2:
+                        quantise_weight_unit(w_grouped, wo_codes, wo_scales, i)
+                    project_and_pool(GROUP * i + t, 1, t == 1 and more_values)
+
+        with tc.psum_pool(name="second", bufs=1) as second_psum:
+            fours = acc[:].rearrange("b (w t) -> b t w", t=4)
+            for g in range(PASSES):
+                flipped = second_psum.tile([P, 4, P], F32, name="attn_flipped%d" % g)
+                for t in range(4):
+                    nc.tensor.transpose(flipped[:, t, :], fours[:, t, g * P : (g + 1) * P], ident[:])
+                grouped = attn_grouped[:, g * 4 * P : (g + 1) * 4 * P]
+                nc.scalar.copy(
+                    out=grouped.rearrange("p (b t) -> p b t", t=4),
+                    in_=flipped[:].rearrange("p t b -> p b t"),
+                )
+                quantise(
+                    grouped, attn_codes[:, g * P : (g + 1) * P], attn_scales[:, g * P : (g + 1) * P]
+                )
+            out_sums = [second_psum.tile([P, N_TILE], F32, name="out_sums%d" % n) for n in range(HALVES)]
+            for g in range(PASSES):
+                for n in range(HALVES):
+                    cols = slice(g * DO + n * N_TILE, g * DO + (n + 1) * N_TILE)
+                    nc.tensor.matmul_mx(
+                        out=out_sums[n][:],
+                        lhsT=attn_codes[:, g * P : (g + 1) * P].bitcast(FP8X4),
+                        lhsT_scale=attn_scales[:, g * P : (g + 1) * P],
+                        rhs=wo_codes[:, cols].bitcast(FP8X4),
+                        rhs_scale=wo_scales[:, cols],
+                        start=(g == 0),
+                        stop=(g == PASSES - 1),
+                    )
+            nc.scalar.copy(out=out_sb[:, 0:N_TILE], in_=out_sums[0][:])
+            nc.sync.dma_start(out=out[:, 0:N_TILE], in_=out_sb[:, 0:N_TILE])
+            nc.vector.tensor_copy(out=out_sb[:, N_TILE:DO], in_=out_sums[1][:])
+            nc.sync.dma_start(out=out[:, N_TILE:DO], in_=out_sb[:, N_TILE:DO])

@@ -33,11 +33,13 @@ def tile_multiheadattention_pb_kernel(tc, values, logw, Wv, Wo, out):
     with ExitStack() as ctx:
         keep = ctx.enter_context(tc.tile_pool(name="keep", bufs=1))
         stage = ctx.enter_context(tc.tile_pool(name="stage", bufs=2))
-        sums_psum = ctx.enter_context(tc.psum_pool(name="sums", bufs=4))
+        banks = ctx.enter_context(tc.psum_pool(name="banks", bufs=8))
         ctx.enter_context(tc.manual_schedule())
 
         ident = keep.tile([P, P], F32)
         make_identity(nc, ident[:])
+        zeros = keep.tile([P, N_TILE], BF16)
+        nc.vector.memset(zeros[:], 0.0)
         acc = keep.tile([P, DP], F32)
         nc.vector.memset(acc[:], 0.0)
         acc_side = keep.tile([P, DP], F32)
@@ -59,67 +61,91 @@ def tile_multiheadattention_pb_kernel(tc, values, logw, Wv, Wo, out):
         attn_scales = keep.tile([P, UNIT_WORDS], U8, align_bytes=64)
         out_sb = keep.tile([P, DO], F32)
 
-        def load_two_units(raw, slot, matrix, unit):
-            src = matrix[unit * P : (unit + 2) * P, :].rearrange("(t p) k -> p t k", p=P)
-            dst = raw[:, slot * DM : (slot + 2) * DM].rearrange("p (t k) -> p t k", t=2)
+        def load_units(raw, slot, matrix, unit, n):
+            src = matrix[unit * P : (unit + n) * P, :].rearrange("(t p) k -> p t k", p=P)
+            dst = raw[:, slot * DM : (slot + n) * DM].rearrange("p (t k) -> p t k", t=n)
             nc.sync.dma_start(out=dst, in_=src)
 
         value_rows = values.flatten_outer_dims()
 
         def load_group(i):
             positions = slice(GROUP * i, GROUP * (i + 1))
+            for t in range(0, GROUP, 2):
+                load_units(x_raw[i], t, value_rows, GROUP * i + t, 2)
             nc.sync.dma_start(
                 out=lw_bf[:, positions, :], in_=logw[positions].rearrange("s b h -> b s h")
             )
-            for t in range(0, GROUP, 2):
-                load_two_units(x_raw[i], t, value_rows, GROUP * i + t)
 
-        for u in range(0, W_UNITS // 2, 2):
-            load_two_units(wv_raw, u, Wv, u)
+        load_units(wv_raw, 0, Wv, 0, 1)
+        load_units(wv_raw, 1, Wv, 1, 1)
+        load_units(wv_raw, 2, Wv, 2, 2)
         load_group(0)
-        for u in range(W_UNITS // 2, W_UNITS, 2):
-            load_two_units(wv_raw, u, Wv, u)
+        load_units(wv_raw, 4, Wv, 4, 2)
+        load_units(wv_raw, 6, Wv, 6, 2)
         for i in range(1, N_GROUPS):
             load_group(i)
             if i % 2 == 1:
-                load_two_units(wo_raw, i - 1, Wo, i - 1)
+                load_units(wo_raw, i - 1, Wo, i - 1, 2)
 
-        def flip_unit(flip_psum, rows, grouped_words):
+        def split_words(copy, raw, split):
+            copy(
+                out=split.bitcast(F32).rearrange("p (u w) -> p u w", u=2),
+                in_=raw.bitcast(F32).rearrange("p (w u) -> p u w", u=2),
+            )
+
+        def flip_unit(copy, rows, grouped_words, split):
             words = rows.bitcast(F32)
-            flipped = flip_psum.tile([P, PASSES, 2, P], F32, tag="flipped")
+            flipped = banks.tile([P, PASSES, 2, P], F32, tag="bank")
             for g in range(PASSES):
                 for u in range(2):
-                    every_2nd = slice(2 * P * g + u, 2 * P * (g + 1), 2)
-                    nc.tensor.transpose(flipped[:, g, u, :], words[:, every_2nd], ident[:])
-            nc.scalar.copy(out=grouped_words, in_=flipped[:].rearrange("p g u r -> p g r u"))
+                    if split:
+                        first = u * UNIT_WORDS + g * P
+                        these = slice(first, first + P)
+                    else:
+                        these = slice(2 * P * g + u, 2 * P * (g + 1), 2)
+                    nc.tensor.transpose(flipped[:, g, u, :], words[:, these], ident[:])
+            copy(out=grouped_words, in_=flipped[:].rearrange("p g u r -> p g r u"))
 
         def quantise(grouped, codes, scales):
             nc.vector.quantize_mx(out=codes.bitcast(FP8X4), scales=scales, in_=grouped)
 
-        def flip_values(flip_psum, i):
-            grouped = stage.tile([P, GROUP * 4 * UNIT_WORDS], BF16, tag="x_grouped", align_bytes=64)
-            words = grouped[:].bitcast(F32).rearrange(
-                "p (t g r u) -> p t g r u", t=GROUP, g=PASSES, u=2
-            )
-            for t in range(GROUP):
-                flip_unit(flip_psum, x_raw[i][:, t * DM : (t + 1) * DM], words[:, t])
-            positions = slice(GROUP * i, GROUP * (i + 1))
-            nc.vector.tensor_copy(out=lw[:, positions, :], in_=lw_bf[:, positions, :])
+        on_vector, on_scalar = nc.vector.tensor_copy, nc.scalar.copy
+
+        def raw_pair(s):
+            first = s % GROUP * DM
+            return x_raw[s // GROUP][:, first : first + 2 * DM]
+
+        def split_pair(s, copies):
+            split = stage.tile([P, 2 * DM], BF16, tag="x_split", bufs=4)
+            parts = []
+            for t in range(2):
+                cols = slice(t * DM, (t + 1) * DM)
+                if copies[t] is None:
+                    parts.append((raw_pair(s)[:, cols], False))
+                else:
+                    split_words(copies[t], raw_pair(s)[:, cols], split[:, cols])
+                    parts.append((split[:, cols], True))
+            return parts
+
+        def flip_pair(parts, copies, split=None):
+            grouped = stage.tile([P, 2 * 4 * UNIT_WORDS], BF16, tag="x_grouped", bufs=4, align_bytes=64)
+            words = grouped[:].bitcast(F32).rearrange("p (t g r u) -> p t g r u", t=2, g=PASSES, u=2)
+            for t in range(2):
+                flip_unit(copies[t], parts[t][0], words[:, t], parts[t][1])
             return grouped
 
-        def quantise_values(grouped, i, pair):
-            n = 2 * UNIT_WORDS
-            first = (GROUP * i + 2 * pair) * UNIT_WORDS
-            quantise(
-                grouped[:, pair * 4 * n : (pair + 1) * 4 * n],
-                val_codes[:, first : first + n],
-                val_scales[:, first : first + n],
-            )
+        def weights_as_floats(i):
+            positions = slice(GROUP * i, GROUP * (i + 1))
+            nc.vector.tensor_copy(out=lw[:, positions, :], in_=lw_bf[:, positions, :])
 
-        def flip_weight_unit(flip_psum, raw, unit):
-            grouped = stage.tile([P, 4 * UNIT_WORDS], BF16, tag="w_grouped", bufs=3, align_bytes=64)
+        def quantise_pair(grouped, s):
+            cols = slice(s * UNIT_WORDS, (s + 2) * UNIT_WORDS)
+            quantise(grouped[:], val_codes[:, cols], val_scales[:, cols])
+
+        def flip_weight_unit(raw, unit, copy):
+            grouped = stage.tile([P, 4 * UNIT_WORDS], BF16, tag="w_grouped", bufs=4, align_bytes=64)
             words = grouped[:].bitcast(F32).rearrange("p (g r u) -> p g r u", g=PASSES, u=2)
-            flip_unit(flip_psum, raw[:, unit * DM : (unit + 1) * DM], words)
+            flip_unit(copy, raw[:, unit * DM : (unit + 1) * DM], words, False)
             return grouped
 
         def quantise_weight_unit(grouped, codes, scales, unit):
@@ -131,8 +157,8 @@ def tile_multiheadattention_pb_kernel(tc, values, logw, Wv, Wo, out):
                     scales[:, first : first + P],
                 )
 
-        def project_and_pool(s, half, on_the_side):
-            vp = sums_psum.tile([P, N_TILE], F32, tag="vp")
+        def project(s, half):
+            vp = banks.tile([P, N_TILE], F32, tag="bank")
             for g in range(PASSES):
                 rows = slice((s * PASSES + g) * P, (s * PASSES + g + 1) * P)
                 cols = slice(g * DP + half * N_TILE, g * DP + (half + 1) * N_TILE)
@@ -145,8 +171,11 @@ def tile_multiheadattention_pb_kernel(tc, values, logw, Wv, Wo, out):
                     start=(g == 0),
                     stop=(g == PASSES - 1),
                 )
+            return vp
+
+        def pool_heads(vp, s, half, on_the_side):
             if on_the_side:
-                weighted = stage.tile([P, N_TILE], F32, tag="weighted")
+                weighted = stage.tile([P, N_TILE], F32, tag="weighted", bufs=3)
             for j in range(HEADS_PER_HALF):
                 h = half * HEADS_PER_HALF + j
                 channels = slice(h * HEAD_DIM, (h + 1) * HEAD_DIM)
@@ -166,69 +195,108 @@ def tile_multiheadattention_pb_kernel(tc, values, logw, Wv, Wo, out):
                     )
             if on_the_side:
                 side = acc_side[:, half * N_TILE : (half + 1) * N_TILE]
-                nc.gpsimd.tensor_tensor(out=side, in0=side, in1=weighted[:], op=ADD)
+                w = N_TILE // 2
+                for c in range(0, N_TILE, w):
+                    nc.gpsimd.tensor_tensor(out=side[:, c : c + w], in0=side[:, c : c + w], in1=weighted[:, c : c + w], op=ADD)
 
         def join_sums(half):
             cols = slice(half * N_TILE, (half + 1) * N_TILE)
             nc.gpsimd.tensor_tensor(out=acc[:, cols], in0=acc[:, cols], in1=acc_side[:, cols], op=ADD)
 
-        with tc.psum_pool(name="flip", bufs=4) as flip_psum:
-            for unit in range(W_UNITS // 2):
-                w_grouped = flip_weight_unit(flip_psum, wv_raw, unit)
-                quantise_weight_unit(w_grouped, wv_codes, wv_scales, unit)
-            x_grouped = flip_values(flip_psum, 0)
-            quantise_values(x_grouped, 0, 0)
-            quantise_values(x_grouped, 0, 1)
-            for unit in range(W_UNITS // 2, W_UNITS):
-                w_grouped = flip_weight_unit(flip_psum, wv_raw, unit)
-                quantise_weight_unit(w_grouped, wv_codes, wv_scales, unit)
+        fours = acc[:].rearrange("b (w t) -> b t w", t=4)
 
-            for i in range(N_GROUPS):
-                more_values = i + 1 < N_GROUPS
-                if not more_values:
-                    join_sums(1)
-                for t in range(GROUP):
-                    project_and_pool(GROUP * i + t, 0, t == 0)
-                if not more_values:
-                    join_sums(0)
-                if more_values:
-                    x_grouped = flip_values(flip_psum, i + 1)
-                w_grouped = flip_weight_unit(flip_psum, wo_raw, i)
-                for t in range(GROUP):
-                    if t < 2 and more_values:
-                        quantise_values(x_grouped, i + 1, t)
-                    if t == 2:
-                        quantise_weight_unit(w_grouped, wo_codes, wo_scales, i)
-                    project_and_pool(GROUP * i + t, 1, t == 1 and more_values)
+        def warm_up(n):
+            for repeat in range(n):
+                scratch = banks.tile([P, N_TILE], F32, tag="bank")
+                nc.tensor.matmul(out=scratch[:], lhsT=zeros[:, 0:P], rhs=zeros[:], start=True, stop=True)
 
-        with tc.psum_pool(name="second", bufs=1) as second_psum:
-            fours = acc[:].rearrange("b (w t) -> b t w", t=4)
-            for g in range(PASSES):
-                flipped = second_psum.tile([P, 4, P], F32, name="attn_flipped%d" % g)
-                for t in range(4):
-                    nc.tensor.transpose(flipped[:, t, :], fours[:, t, g * P : (g + 1) * P], ident[:])
-                grouped = attn_grouped[:, g * 4 * P : (g + 1) * 4 * P]
-                nc.scalar.copy(
-                    out=grouped.rearrange("p (b t) -> p b t", t=4),
-                    in_=flipped[:].rearrange("p t b -> p b t"),
+        def flip_attn(g):
+            flipped = banks.tile([P, 4, P], F32, tag="bank")
+            for t in range(4):
+                nc.tensor.transpose(flipped[:, t, :], fours[:, t, g * P : (g + 1) * P], ident[:])
+            grouped = attn_grouped[:, g * 4 * P : (g + 1) * 4 * P]
+            nc.scalar.copy(
+                out=grouped.rearrange("p (b t) -> p b t", t=4),
+                in_=flipped[:].rearrange("p t b -> p b t"),
+            )
+            quantise(grouped, attn_codes[:, g * P : (g + 1) * P], attn_scales[:, g * P : (g + 1) * P])
+
+        V, S = nc.vector.tensor_copy, nc.scalar.copy
+
+        grouped_w = {}
+        x_split = {}
+        x_grouped = {}
+        for unit in range(4):
+            grouped_w[unit] = flip_weight_unit(wv_raw, unit, S)
+            if unit > 0:
+                quantise_weight_unit(grouped_w[unit - 1], wv_codes, wv_scales, unit - 1)
+        x_split[0] = split_pair(0, (None, None))
+        x_grouped[0] = flip_pair(x_split[0], (V, S), True)
+        quantise_weight_unit(grouped_w[3], wv_codes, wv_scales, 3)
+        x_split[2] = split_pair(2, (None, None))
+        x_grouped[2] = flip_pair(x_split[2], (V, S), True)
+        quantise_pair(x_grouped[0], 0)
+        weights_as_floats(0)
+        quantise_pair(x_grouped[2], 2)
+
+        steps = []
+        for j in range(16):
+            if j in (0, 1):
+                step_banks = [(s, j) for s in range(4)]
+            elif j in (14, 15):
+                step_banks = [(s, j - 14) for s in range(28, 32)]
+            else:
+                step_banks = [(s, half) for s in (2 * j, 2 * j + 1) for half in range(2)]
+            pair = 2 * j + 4 if j < 14 else None
+            wo = {1: 0, 3: 1, 5: 2, 7: 3, 9: 4, 11: 5, 12: 6, 13: 7}.get(j)
+            side = ((),(),(0,),(),(0,),(),(0,),(),(0,),(),(0,),(),(0,),(0,2,),(0,1,),(),)[j]
+            steps.append((step_banks, pair, wo, side))
+
+        w_grouped = None
+        for j, (step_banks, pair, wo, side) in enumerate(steps):
+            if j == 0:
+                x_split[4] = split_pair(4, (S, S))
+            elif j + 1 < 14:
+                x_split[2 * j + 6] = split_pair(2 * j + 6, ((S, S),)[j % 1])
+            for n, (s, half) in enumerate(step_banks):
+                if n == 0 and j >= 1 and j < 15 and 2 * j + 2 < 32:
+                    quantise_pair(x_grouped[2 * j + 2], 2 * j + 2)
+                    if j % 2 == 1:
+                        weights_as_floats((2 * j + 2) // 4)
+                if n == 2 and w_grouped is not None:
+                    quantise_weight_unit(w_grouped[0], wo_codes, wo_scales, w_grouped[1])
+                    w_grouped = None
+                pool_heads(project(s, half), s, half, n in side)
+                if (j, n) == (15,0): join_sums(0)
+            if j == 0:
+                for unit in range(4, 8):
+                    grouped_w[unit] = flip_weight_unit(wv_raw, unit, (V, S)[unit % 2])
+                    if unit > 4:
+                        quantise_weight_unit(grouped_w[unit - 1], wv_codes, wv_scales, unit - 1)
+                x_split[6] = split_pair(6, (S, S))
+            if pair is not None:
+                x_grouped[pair] = flip_pair(x_split[pair], (S, S), True)
+            if j == 0:
+                quantise_weight_unit(grouped_w[7], wv_codes, wv_scales, 7)
+            if wo is not None:
+                w_grouped = (flip_weight_unit(wo_raw, wo, S), wo)
+
+        flip_attn(0)
+        flip_attn(1)
+        out_sums = [banks.tile([P, N_TILE], F32, tag="bank", name="out_sums%d" % n) for n in range(HALVES)]
+        for g in range(PASSES):
+            for n in range(HALVES):
+                cols = slice(g * DO + n * N_TILE, g * DO + (n + 1) * N_TILE)
+                nc.tensor.matmul_mx(
+                    out=out_sums[n][:],
+                    lhsT=attn_codes[:, g * P : (g + 1) * P].bitcast(FP8X4),
+                    lhsT_scale=attn_scales[:, g * P : (g + 1) * P],
+                    rhs=wo_codes[:, cols].bitcast(FP8X4),
+                    rhs_scale=wo_scales[:, cols],
+                    start=(g == 0),
+                    stop=(g == PASSES - 1),
                 )
-                quantise(
-                    grouped, attn_codes[:, g * P : (g + 1) * P], attn_scales[:, g * P : (g + 1) * P]
-                )
-            out_sums = [second_psum.tile([P, N_TILE], F32, name="out_sums%d" % n) for n in range(HALVES)]
-            for g in range(PASSES):
-                for n in range(HALVES):
-                    cols = slice(g * DO + n * N_TILE, g * DO + (n + 1) * N_TILE)
-                    nc.tensor.matmul_mx(
-                        out=out_sums[n][:],
-                        lhsT=attn_codes[:, g * P : (g + 1) * P].bitcast(FP8X4),
-                        lhsT_scale=attn_scales[:, g * P : (g + 1) * P],
-                        rhs=wo_codes[:, cols].bitcast(FP8X4),
-                        rhs_scale=wo_scales[:, cols],
-                        start=(g == 0),
-                        stop=(g == PASSES - 1),
-                    )
-            nc.scalar.copy(out=out_sb[:, 0:N_TILE], in_=out_sums[0][:])
-            nc.sync.dma_start(out=out[:, 0:N_TILE], in_=out_sb[:, 0:N_TILE])
-            nc.vector.tensor_copy(out=out_sb[:, N_TILE:DO], in_=out_sums[1][:])
-            nc.sync.dma_start(out=out[:, N_TILE:DO], in_=out_sb[:, N_TILE:DO])
+        nc.scalar.copy(out=out_sb[:, 0:N_TILE], in_=out_sums[0][:])
+        nc.sync.dma_start(out=out[:, 0:N_TILE], in_=out_sb[:, 0:N_TILE])
+        nc.vector.tensor_copy(out=out_sb[:, N_TILE:DO], in_=out_sums[1][:])
+        nc.sync.dma_start(out=out[:, N_TILE:DO], in_=out_sb[:, N_TILE:DO])

@@ -142,8 +142,19 @@ def tile_multiheadattention_pb_kernel(tc, values, logw, Wv, Wo, out):
             cols = slice(s * UNIT_WORDS, (s + 2) * UNIT_WORDS)
             quantise(grouped[:], val_codes[:, cols], val_scales[:, cols])
 
+        def split_weight_unit(raw, unit, copy):
+            split = stage.tile([P, DM], BF16, tag="w_split", bufs=4)
+            split_words(copy, raw[:, unit * DM : (unit + 1) * DM], split[:])
+            return split
+
+        def flip_split_weight_unit(split, copy):
+            grouped = stage.tile([P, 4 * UNIT_WORDS], BF16, tag="w_grouped", bufs=5, align_bytes=64)
+            words = grouped[:].bitcast(F32).rearrange("p (g r u) -> p g r u", g=PASSES, u=2)
+            flip_unit(copy, split[:], words, True)
+            return grouped
+
         def flip_weight_unit(raw, unit, copy):
-            grouped = stage.tile([P, 4 * UNIT_WORDS], BF16, tag="w_grouped", bufs=4, align_bytes=64)
+            grouped = stage.tile([P, 4 * UNIT_WORDS], BF16, tag="w_grouped", bufs=5, align_bytes=64)
             words = grouped[:].bitcast(F32).rearrange("p (g r u) -> p g r u", g=PASSES, u=2)
             flip_unit(copy, raw[:, unit * DM : (unit + 1) * DM], words, False)
             return grouped
@@ -223,70 +234,116 @@ def tile_multiheadattention_pb_kernel(tc, values, logw, Wv, Wo, out):
 
         V, S = nc.vector.tensor_copy, nc.scalar.copy
 
+        def split_group(i, copies):
+            return [split_pair(4 * i, copies[0:2]), split_pair(4 * i + 2, copies[2:4])]
+
+        def flip_group(parts, copies):
+            return [flip_pair(parts[0], copies[0:2]), flip_pair(parts[1], copies[2:4])]
+
+        def flip_weights(units, copies):
+            return [(unit, flip_weight_unit(wo_raw, unit, copies[n])) for n, unit in enumerate(units)]
+
+        raw4 = (None, None, None, None)
         grouped_w = {}
-        x_split = {}
-        x_grouped = {}
+        warm_up(5)
+        pending = []
+
+        def settle(keep_back):
+            while len(pending) > keep_back:
+                what = pending[0]
+                pending.remove(what)
+                if what[0] == "w":
+                    quantise_weight_unit(what[2], wv_codes, wv_scales, what[1])
+                else:
+                    quantise_pair(what[2], what[1])
+
+        cw = (S,S,S,S,S,S,S,S)
+        dm = (1,1,1,1,)
+        dx = (1,1,0,0,)
+
+        def w_unit(unit, copy):
+            split = split_weight_unit(wv_raw, unit, V)
+            pending.append(("w", unit, flip_split_weight_unit(split, copy)))
+
+        def x_pair(s, splits, copies, dummies):
+            grouped = stage.tile([P, 2 * 4 * UNIT_WORDS], BF16, tag="x_grouped", bufs=4, align_bytes=64)
+            words = grouped[:].bitcast(F32).rearrange("p (t g r u) -> p t g r u", t=2, g=PASSES, u=2)
+            split = stage.tile([P, 2 * DM], BF16, tag="x_split", bufs=4)
+            for t in range(2):
+                cols = slice(t * DM, (t + 1) * DM)
+                if splits[t] is None:
+                    flip_unit(copies[t], raw_pair(s)[:, cols], words[:, t], False)
+                else:
+                    split_words(splits[t], raw_pair(s)[:, cols], split[:, cols])
+                    flip_unit(copies[t], split[:, cols], words[:, t], True)
+                warm_up(dummies[t])
+            pending.append(("x", s, grouped))
+
         for unit in range(4):
-            grouped_w[unit] = flip_weight_unit(wv_raw, unit, S)
-            if unit > 0:
-                quantise_weight_unit(grouped_w[unit - 1], wv_codes, wv_scales, unit - 1)
-        x_split[0] = split_pair(0, (None, None))
-        x_grouped[0] = flip_pair(x_split[0], (V, S), True)
-        quantise_weight_unit(grouped_w[3], wv_codes, wv_scales, 3)
-        x_split[2] = split_pair(2, (None, None))
-        x_grouped[2] = flip_pair(x_split[2], (V, S), True)
-        quantise_pair(x_grouped[0], 0)
+            w_unit(unit, cw[unit])
+            warm_up(dm[unit])
+            settle(2)
+        x_pair(0, (V, V), (S,S), dx[0:2])
+        settle(2)
+        x_pair(2, (V, V), (S,S), dx[2:4])
         weights_as_floats(0)
-        quantise_pair(x_grouped[2], 2)
-
-        steps = []
-        for j in range(16):
-            if j in (0, 1):
-                step_banks = [(s, j) for s in range(4)]
-            elif j in (14, 15):
-                step_banks = [(s, j - 14) for s in range(28, 32)]
-            else:
-                step_banks = [(s, half) for s in (2 * j, 2 * j + 1) for half in range(2)]
-            pair = 2 * j + 4 if j < 14 else None
-            wo = {1: 0, 3: 1, 5: 2, 7: 3, 9: 4, 11: 5, 12: 6, 13: 7}.get(j)
-            side = ((),(),(0,),(),(0,),(),(0,),(),(0,),(),(0,),(),(0,),(0,2,),(0,1,),(),)[j]
-            steps.append((step_banks, pair, wo, side))
-
-        w_grouped = None
-        for j, (step_banks, pair, wo, side) in enumerate(steps):
-            if j == 0:
-                x_split[4] = split_pair(4, (S, S))
-            elif j + 1 < 14:
-                x_split[2 * j + 6] = split_pair(2 * j + 6, ((S, S),)[j % 1])
-            for n, (s, half) in enumerate(step_banks):
-                if n == 0 and j >= 1 and j < 15 and 2 * j + 2 < 32:
-                    quantise_pair(x_grouped[2 * j + 2], 2 * j + 2)
-                    if j % 2 == 1:
-                        weights_as_floats((2 * j + 2) // 4)
-                if n == 2 and w_grouped is not None:
-                    quantise_weight_unit(w_grouped[0], wo_codes, wo_scales, w_grouped[1])
-                    w_grouped = None
+        settle(0)
+        x_split = split_group(1, (S,S,S,S))
+        w_split = [split_weight_unit(wv_raw, unit, V) for unit in range(4, 8)]
+        for s in range(4):
+            pool_heads(project(s, 0), s, 0, s in ())
+        for unit in range(4, 8):
+            pending.append(("w", unit, flip_split_weight_unit(w_split[unit - 4], cw[unit])))
+            settle(1)
+        x_now = flip_group(x_split, (S,S,S,S))
+        settle(0)
+        pending.extend([("x", 4, x_now[0]), ("x", 6, x_now[1])])
+        weights_as_floats(1)
+        warm_up(0)
+        for s in range(4):
+            if s == 0:
+                x_split = split_group(2, (V,V,V,V))
+            if s == 1:
+                settle(1)
+            if s == 2:
+                settle(0)
+            pool_heads(project(s, 1), s, 1, False)
+        wo_units = {0:(0,),1:(1,),2:(2,),3:(3,),4:(4,),5:(5,),6:(6,7,)}
+        sides = {}
+        x_now = flip_group(x_split, (S,S,S,S))
+        w_now = flip_weights(wo_units.get(0, ()), (S, S))
+        for i in range(1, 8):
+            order = [(4 * i + t, half) for t in range(4) for half in range(2)]
+            if i == 7:
+                order = [(4 * i + t, half) for half in range(2) for t in range(4)]
+            side = (1,) if i == 7 else (0,2,) if i == 6 else sides.get(i, (0,4,))
+            for n, (s, half) in enumerate(order):
+                if i < 7:
+                    if n == 0:
+                        quantise_pair(x_now[0], 4 * i + 4)
+                    if n == 1:
+                        quantise_pair(x_now[1], 4 * i + 6)
+                        weights_as_floats(i + 1)
+                if n == 2:
+                    for unit, grouped in w_now:
+                        quantise_weight_unit(grouped, wo_codes, wo_scales, unit)
+                    w_now = []
                 pool_heads(project(s, half), s, half, n in side)
-                if (j, n) == (15,0): join_sums(0)
-            if j == 0:
-                for unit in range(4, 8):
-                    grouped_w[unit] = flip_weight_unit(wv_raw, unit, (V, S)[unit % 2])
-                    if unit > 4:
-                        quantise_weight_unit(grouped_w[unit - 1], wv_codes, wv_scales, unit - 1)
-                x_split[6] = split_pair(6, (S, S))
-            if pair is not None:
-                x_grouped[pair] = flip_pair(x_split[pair], (S, S), True)
-            if j == 0:
-                quantise_weight_unit(grouped_w[7], wv_codes, wv_scales, 7)
-            if wo is not None:
-                w_grouped = (flip_weight_unit(wo_raw, wo, S), wo)
+                if n == 1 and i + 2 < 8:
+                    x_split = split_group(i + 2, (S,S,S,S))
+                if i == 7 and n == 4:
+                    join_sums(0)
+            if i + 2 < 8:
+                x_now = flip_group(x_split, (S,S,S,S))
+            w_now = flip_weights(wo_units.get(i, ()), (S, S))
 
         flip_attn(0)
         flip_attn(1)
-        out_sums = [banks.tile([P, N_TILE], F32, tag="bank", name="out_sums%d" % n) for n in range(HALVES)]
+        quarter = DO // 4
+        out_sums = [banks.tile([P, quarter], F32, tag="bank", name="out_sums%d" % n) for n in range(4)]
         for g in range(PASSES):
-            for n in range(HALVES):
-                cols = slice(g * DO + n * N_TILE, g * DO + (n + 1) * N_TILE)
+            for n in range(4):
+                cols = slice(g * DO + n * quarter, g * DO + (n + 1) * quarter)
                 nc.tensor.matmul_mx(
                     out=out_sums[n][:],
                     lhsT=attn_codes[:, g * P : (g + 1) * P].bitcast(FP8X4),
@@ -296,7 +353,7 @@ def tile_multiheadattention_pb_kernel(tc, values, logw, Wv, Wo, out):
                     start=(g == 0),
                     stop=(g == PASSES - 1),
                 )
-        nc.scalar.copy(out=out_sb[:, 0:N_TILE], in_=out_sums[0][:])
-        nc.sync.dma_start(out=out[:, 0:N_TILE], in_=out_sb[:, 0:N_TILE])
-        nc.vector.tensor_copy(out=out_sb[:, N_TILE:DO], in_=out_sums[1][:])
-        nc.sync.dma_start(out=out[:, N_TILE:DO], in_=out_sb[:, N_TILE:DO])
+        for n in range(4):
+            cols = slice(n * quarter, (n + 1) * quarter)
+            (S, V)[n % 2](out=out_sb[:, cols], in_=out_sums[n][:])
+            nc.sync.dma_start(out=out[:, cols], in_=out_sb[:, cols])

@@ -143,18 +143,18 @@ def tile_multiheadattention_pb_kernel(tc, values, logw, Wv, Wo, out):
             quantise(grouped[:], val_codes[:, cols], val_scales[:, cols])
 
         def split_weight_unit(raw, unit, copy):
-            split = stage.tile([P, DM], BF16, tag="w_split", bufs=4)
+            split = stage.tile([P, DM], BF16, tag="w_split", bufs=6)
             split_words(copy, raw[:, unit * DM : (unit + 1) * DM], split[:])
             return split
 
         def flip_split_weight_unit(split, copy):
-            grouped = stage.tile([P, 4 * UNIT_WORDS], BF16, tag="w_grouped", bufs=5, align_bytes=64)
+            grouped = stage.tile([P, 4 * UNIT_WORDS], BF16, tag="w_grouped", bufs=6, align_bytes=64)
             words = grouped[:].bitcast(F32).rearrange("p (g r u) -> p g r u", g=PASSES, u=2)
             flip_unit(copy, split[:], words, True)
             return grouped
 
         def flip_weight_unit(raw, unit, copy):
-            grouped = stage.tile([P, 4 * UNIT_WORDS], BF16, tag="w_grouped", bufs=5, align_bytes=64)
+            grouped = stage.tile([P, 4 * UNIT_WORDS], BF16, tag="w_grouped", bufs=6, align_bytes=64)
             words = grouped[:].bitcast(F32).rearrange("p (g r u) -> p g r u", g=PASSES, u=2)
             flip_unit(copy, raw[:, unit * DM : (unit + 1) * DM], words, False)
             return grouped
@@ -308,34 +308,51 @@ def tile_multiheadattention_pb_kernel(tc, values, logw, Wv, Wo, out):
             if s == 2:
                 settle(0)
             pool_heads(project(s, 1), s, 1, False)
-        wo_units = {0:(0,),1:(1,),2:(2,),3:(3,),4:(4,),5:(5,),6:(6,7,)}
         sides = {}
-        x_now = flip_group(x_split, (S,S,S,S))
-        w_now = flip_weights(wo_units.get(0, ()), (S, S))
+        wo_runs = [(5, 4, (0,1,2,3,)), (6, 8, (4,5,6,7,))]
+        wo_splits = [(2, 6, (0,)), (3, 6, (1,)), (4, 6, (2,)), (5, 0, (3,)), (5, 6, (4,)), (6, 2, (5,6,7,))]
+        wo_quants = [(6, 0, (0,1,2,3,)), (7, 0, (4,5,6,7,))]
+        wd = (S,S,S,S)
+        wc = (S,S,S,S)
+        wo_split = {}
+        wo_grouped = {}
+
+        def wo_events(i, n):
+            for r, m, units in wo_splits:
+                if (r, m) == (i, n):
+                    for u in units:
+                        wo_split[u] = split_weight_unit(wo_raw, u, wd[u % 4])
+            for r, m, units in wo_runs:
+                if (r, m) == (i, n):
+                    for u in units:
+                        wo_grouped[u] = flip_split_weight_unit(wo_split[u], wc[u % 4])
+            for r, m, units in wo_quants:
+                if (r, m) == (i, n):
+                    for u in units:
+                        quantise_weight_unit(wo_grouped[u], wo_codes, wo_scales, u)
+
+        x_now = flip_group(x_split, (S, S, S, S))
         for i in range(1, 8):
             order = [(4 * i + t, half) for t in range(4) for half in range(2)]
             if i == 7:
                 order = [(4 * i + t, half) for half in range(2) for t in range(4)]
-            side = (1,) if i == 7 else (0,2,) if i == 6 else sides.get(i, (0,4,))
+            side = (2,) if i == 7 else (2,4,) if i == 6 else sides.get(i, (2,))
             for n, (s, half) in enumerate(order):
+                wo_events(i, n)
                 if i < 7:
                     if n == 0:
                         quantise_pair(x_now[0], 4 * i + 4)
                     if n == 1:
                         quantise_pair(x_now[1], 4 * i + 6)
                         weights_as_floats(i + 1)
-                if n == 2:
-                    for unit, grouped in w_now:
-                        quantise_weight_unit(grouped, wo_codes, wo_scales, unit)
-                    w_now = []
                 pool_heads(project(s, half), s, half, n in side)
                 if n == 1 and i + 2 < 8:
-                    x_split = split_group(i + 2, (S,S,S,S))
+                    x_split = split_group(i + 2, (S, S, S, S))
                 if i == 7 and n == 4:
                     join_sums(0)
             if i + 2 < 8:
-                x_now = flip_group(x_split, (S,S,S,S))
-            w_now = flip_weights(wo_units.get(i, ()), (S, S))
+                x_now = flip_group(x_split, (S, S, S, S))
+            wo_events(i, 8)
 
         flip_attn(0)
         flip_attn(1)

@@ -136,21 +136,21 @@ def tile_multiheadattention_pb_kernel(tc, values, logw, Wv, Wo, out):
 
         def weights_as_floats(i):
             positions = slice(GROUP * i, GROUP * (i + 1))
-            nc.vector.tensor_copy(out=lw[:, positions, :], in_=lw_bf[:, positions, :])
+            nc.scalar.copy(out=lw[:, positions, :], in_=lw_bf[:, positions, :])
 
         def quantise_pair(grouped, s):
             cols = slice(s * UNIT_WORDS, (s + 2) * UNIT_WORDS)
             quantise(grouped[:], val_codes[:, cols], val_scales[:, cols])
 
         def split_weight_unit(raw, unit, copy):
-            split = stage.tile([P, DM], BF16, tag="w_split", bufs=6)
+            split = stage.tile([P, DM], BF16, tag="w_split", bufs=4)
             split_words(copy, raw[:, unit * DM : (unit + 1) * DM], split[:])
             return split
 
         def flip_split_weight_unit(split, copy):
             grouped = stage.tile([P, 4 * UNIT_WORDS], BF16, tag="w_grouped", bufs=6, align_bytes=64)
             words = grouped[:].bitcast(F32).rearrange("p (g r u) -> p g r u", g=PASSES, u=2)
-            flip_unit(copy, split[:], words, True)
+            flip_unit(copy, split, words, True)
             return grouped
 
         def flip_weight_unit(raw, unit, copy):
@@ -243,75 +243,114 @@ def tile_multiheadattention_pb_kernel(tc, values, logw, Wv, Wo, out):
         def flip_weights(units, copies):
             return [(unit, flip_weight_unit(wo_raw, unit, copies[n])) for n, unit in enumerate(units)]
 
-        raw4 = (None, None, None, None)
-        grouped_w = {}
+        w_split, w_grp, x_split_t, x_grp = {}, {}, {}, {}
+
+        def quantise_position(s):
+            cols = slice(s * UNIT_WORDS, (s + 1) * UNIT_WORDS)
+            grouped = x_grp[s // 2][:, s % 2 * 4 * UNIT_WORDS : (s % 2 + 1) * 4 * UNIT_WORDS]
+            quantise(grouped, val_codes[:, cols], val_scales[:, cols])
+
+        def flip_position(s, copy):
+            if s % 2 == 0:
+                x_grp[s // 2] = stage.tile([P, 2 * 4 * UNIT_WORDS], BF16, tag="x_grouped", bufs=4, align_bytes=64, name="x_grouped")
+            words = x_grp[s // 2][:].bitcast(F32).rearrange("p (t g r u) -> p t g r u", t=2, g=PASSES, u=2)
+            raw = raw_pair(s // 2 * 2)[:, s % 2 * DM : (s % 2 + 1) * DM]
+            if s in x_split_t:
+                flip_unit(copy, x_split_t[s], words[:, s % 2], True)
+            else:
+                flip_unit(copy, raw, words[:, s % 2], False)
+
+        def split_position(s, copy):
+            if s % 2 == 0:
+                x_split_t["pair"] = stage.tile([P, 2 * DM], BF16, tag="x_split", bufs=4, name="x_split")
+            part = x_split_t["pair"][:, s % 2 * DM : (s % 2 + 1) * DM]
+            split_words(copy, raw_pair(s // 2 * 2)[:, s % 2 * DM : (s % 2 + 1) * DM], part)
+            x_split_t[s] = part
+
+        def flip_w(u, copy):
+            if u in w_split:
+                w_grp[u] = flip_split_weight_unit(w_split[u][:], copy)
+            else:
+                w_grp[u] = flip_weight_unit(wv_raw, u, copy)
+
+        def bank(s, half):
+            pool_heads(project(s, half), s, half, False)
+
+        vps = {}
         warm_up(5)
-        pending = []
-
-        def settle(keep_back):
-            while len(pending) > keep_back:
-                what = pending[0]
-                pending.remove(what)
-                if what[0] == "w":
-                    quantise_weight_unit(what[2], wv_codes, wv_scales, what[1])
-                else:
-                    quantise_pair(what[2], what[1])
-
-        cw = (S,S,S,S,S,S,S,S)
-        dm = (1,1,1,1,)
-        dx = (1,1,0,0,)
-
-        def w_unit(unit, copy):
-            split = split_weight_unit(wv_raw, unit, V)
-            pending.append(("w", unit, flip_split_weight_unit(split, copy)))
-
-        def x_pair(s, splits, copies, dummies):
-            grouped = stage.tile([P, 2 * 4 * UNIT_WORDS], BF16, tag="x_grouped", bufs=4, align_bytes=64)
-            words = grouped[:].bitcast(F32).rearrange("p (t g r u) -> p t g r u", t=2, g=PASSES, u=2)
-            split = stage.tile([P, 2 * DM], BF16, tag="x_split", bufs=4)
-            for t in range(2):
-                cols = slice(t * DM, (t + 1) * DM)
-                if splits[t] is None:
-                    flip_unit(copies[t], raw_pair(s)[:, cols], words[:, t], False)
-                else:
-                    split_words(splits[t], raw_pair(s)[:, cols], split[:, cols])
-                    flip_unit(copies[t], split[:, cols], words[:, t], True)
-                warm_up(dummies[t])
-            pending.append(("x", s, grouped))
-
-        for unit in range(4):
-            w_unit(unit, cw[unit])
-            warm_up(dm[unit])
-            settle(2)
-        x_pair(0, (V, V), (S,S), dx[0:2])
-        settle(2)
-        x_pair(2, (V, V), (S,S), dx[2:4])
+        w_split[0] = split_weight_unit(wv_raw, 0, V)
+        flip_w(0, S)
+        w_split[1] = split_weight_unit(wv_raw, 1, V)
+        warm_up(1)
+        flip_w(1, S)
+        w_split[2] = split_weight_unit(wv_raw, 2, V)
+        warm_up(1)
+        quantise_weight_unit(w_grp[0], wv_codes, wv_scales, 0)
+        flip_w(2, S)
+        w_split[3] = split_weight_unit(wv_raw, 3, V)
+        quantise_weight_unit(w_grp[1], wv_codes, wv_scales, 1)
+        flip_w(3, S)
+        warm_up(1)
+        split_position(0, V)
+        quantise_weight_unit(w_grp[2], wv_codes, wv_scales, 2)
+        flip_position(0, S)
+        split_position(1, V)
+        warm_up(1)
+        flip_position(1, S)
+        split_position(2, V)
+        warm_up(1)
+        flip_position(2, S)
+        split_position(3, V)
+        quantise_weight_unit(w_grp[3], wv_codes, wv_scales, 3)
+        flip_position(3, S)
+        quantise_position(0)
         weights_as_floats(0)
-        settle(0)
-        x_split = split_group(1, (S,S,S,S))
-        w_split = [split_weight_unit(wv_raw, unit, V) for unit in range(4, 8)]
-        for s in range(4):
-            pool_heads(project(s, 0), s, 0, s in ())
-        for unit in range(4, 8):
-            pending.append(("w", unit, flip_split_weight_unit(w_split[unit - 4], cw[unit])))
-            settle(1)
-        x_now = flip_group(x_split, (S,S,S,S))
-        settle(0)
-        pending.extend([("x", 4, x_now[0]), ("x", 6, x_now[1])])
+        w_split[4] = split_weight_unit(wv_raw, 4, V)
+        quantise_position(1)
+        w_split[5] = split_weight_unit(wv_raw, 5, V)
+        vps[0, 0] = project(0, 0)
+        vps[1, 0] = project(1, 0)
+        quantise_position(2)
+        w_split[6] = split_weight_unit(wv_raw, 6, V)
+        quantise_position(3)
+        w_split[7] = split_weight_unit(wv_raw, 7, V)
+        split_position(4, S)
+        split_position(5, S)
+        flip_w(4, S)
+        flip_w(5, S)
+        flip_w(6, S)
+        flip_w(7, S)
+        pool_heads(vps[0, 0], 0, 0, False)
+        pool_heads(vps[1, 0], 1, 0, False)
+        vps[2, 0] = project(2, 0)
+        vps[3, 0] = project(3, 0)
+        quantise_weight_unit(w_grp[4], wv_codes, wv_scales, 4)
+        pool_heads(vps[2, 0], 2, 0, False)
+        quantise_weight_unit(w_grp[5], wv_codes, wv_scales, 5)
+        pool_heads(vps[3, 0], 3, 0, False)
+        flip_position(4, S)
+        flip_position(5, S)
+        flip_position(6, S)
+        flip_position(7, S)
+        warm_up(2)
+        quantise_weight_unit(w_grp[6], wv_codes, wv_scales, 6)
+        quantise_weight_unit(w_grp[7], wv_codes, wv_scales, 7)
         weights_as_floats(1)
-        warm_up(0)
-        for s in range(4):
-            if s == 0:
-                x_split = split_group(2, (V,V,V,V))
-            if s == 1:
-                settle(1)
-            if s == 2:
-                settle(0)
-            pool_heads(project(s, 1), s, 1, False)
+        x_split = split_group(2, (V, V, V, V))
+        vps[0, 1] = project(0, 1)
+        pool_heads(vps[0, 1], 0, 1, False)
+        vps[1, 1] = project(1, 1)
+        quantise_pair(x_grp[4 // 2], 4)
+        pool_heads(vps[1, 1], 1, 1, False)
+        vps[2, 1] = project(2, 1)
+        quantise_pair(x_grp[6 // 2], 6)
+        pool_heads(vps[2, 1], 2, 1, False)
+        vps[3, 1] = project(3, 1)
+        pool_heads(vps[3, 1], 3, 1, False)
         sides = {}
-        wo_runs = [(5, 4, (0,1,2,3,)), (6, 8, (4,5,6,7,))]
-        wo_splits = [(2, 6, (0,)), (3, 6, (1,)), (4, 6, (2,)), (5, 0, (3,)), (5, 6, (4,)), (6, 2, (5,6,7,))]
-        wo_quants = [(6, 0, (0,1,2,3,)), (7, 0, (4,5,6,7,))]
+        wo_runs = [(4, 4, (0,1,2,3,)), (5, 4, (4,5,6,7,))]
+        wo_splits = [(1, 5, (0,)), (1, 7, (1,)), (2, 5, (2,)), (2, 7, (3,)), (3, 5, (4,)), (3, 7, (5,)), (4, 5, (6,)), (4, 7, (7,))]
+        wo_quants = [(5, 0, (0,1,2,3,)), (6, 0, (4,5,6,7,))]
         wd = (S,S,S,S)
         wc = (S,S,S,S)
         wo_split = {}
@@ -321,7 +360,8 @@ def tile_multiheadattention_pb_kernel(tc, values, logw, Wv, Wo, out):
             for r, m, units in wo_splits:
                 if (r, m) == (i, n):
                     for u in units:
-                        wo_split[u] = split_weight_unit(wo_raw, u, wd[u % 4])
+                        wo_split[u] = wv_raw[:, u * DM : (u + 1) * DM]
+                        split_words(wd[u % 4], wo_raw[:, u * DM : (u + 1) * DM], wo_split[u])
             for r, m, units in wo_runs:
                 if (r, m) == (i, n):
                     for u in units:
@@ -336,7 +376,7 @@ def tile_multiheadattention_pb_kernel(tc, values, logw, Wv, Wo, out):
             order = [(4 * i + t, half) for t in range(4) for half in range(2)]
             if i == 7:
                 order = [(4 * i + t, half) for half in range(2) for t in range(4)]
-            side = (2,) if i == 7 else (2,4,) if i == 6 else sides.get(i, (2,))
+            side = (0,) if i == 7 else (0,2,4,) if i == 6 else sides.get(i, (2,))
             for n, (s, half) in enumerate(order):
                 wo_events(i, n)
                 if i < 7:
@@ -348,17 +388,16 @@ def tile_multiheadattention_pb_kernel(tc, values, logw, Wv, Wo, out):
                 pool_heads(project(s, half), s, half, n in side)
                 if n == 1 and i + 2 < 8:
                     x_split = split_group(i + 2, (S, S, S, S))
-                if i == 7 and n == 4:
+                if i == 7 and n == 5:
                     join_sums(0)
             if i + 2 < 8:
                 x_now = flip_group(x_split, (S, S, S, S))
             wo_events(i, 8)
 
-        flip_attn(0)
-        flip_attn(1)
         quarter = DO // 4
         out_sums = [banks.tile([P, quarter], F32, tag="bank", name="out_sums%d" % n) for n in range(4)]
-        for g in range(PASSES):
+
+        def project_out(g):
             for n in range(4):
                 cols = slice(g * DO + n * quarter, g * DO + (n + 1) * quarter)
                 nc.tensor.matmul_mx(
@@ -370,6 +409,11 @@ def tile_multiheadattention_pb_kernel(tc, values, logw, Wv, Wo, out):
                     start=(g == 0),
                     stop=(g == PASSES - 1),
                 )
+
+        flip_attn(0)
+        flip_attn(1)
+        project_out(0)
+        project_out(1)
         for n in range(4):
             cols = slice(n * quarter, (n + 1) * quarter)
             (S, V)[n % 2](out=out_sb[:, cols], in_=out_sums[n][:])

@@ -32,9 +32,10 @@ def tile_multiheadattention_pb_kernel(tc, values, logw, Wv, Wo, out):
     nc = tc.nc
     with ExitStack() as ctx:
         keep = ctx.enter_context(tc.tile_pool(name="keep", bufs=1))
-        stage = ctx.enter_context(tc.tile_pool(name="stage", bufs=2))
+        stage = ctx.enter_context(tc.tile_pool(name="stage", bufs=4))
         banks = ctx.enter_context(tc.psum_pool(name="banks", bufs=8))
         ctx.enter_context(tc.manual_schedule())
+        V, S = nc.vector.tensor_copy, nc.scalar.copy
 
         ident = keep.tile([P, P], F32)
         make_identity(nc, ident[:])
@@ -56,6 +57,7 @@ def tile_multiheadattention_pb_kernel(tc, values, logw, Wv, Wo, out):
         wv_scales = keep.tile([P, PASSES * DP], U8, align_bytes=64)
         wo_codes = keep.tile([P, PASSES * DO], U32, align_bytes=64)
         wo_scales = keep.tile([P, PASSES * DO], U8, align_bytes=64)
+        attn = keep.tile([P, DP], BF16)
         attn_grouped = keep.tile([P, 4 * UNIT_WORDS], BF16, align_bytes=64)
         attn_codes = keep.tile([P, UNIT_WORDS], U32, align_bytes=64)
         attn_scales = keep.tile([P, UNIT_WORDS], U8, align_bytes=64)
@@ -68,10 +70,11 @@ def tile_multiheadattention_pb_kernel(tc, values, logw, Wv, Wo, out):
 
         value_rows = values.flatten_outer_dims()
 
-        def load_group(i):
+        def load_pair(s):
+            load_units(x_raw[s // GROUP], s % GROUP, value_rows, s, 2)
+
+        def load_logw(i):
             positions = slice(GROUP * i, GROUP * (i + 1))
-            for t in range(0, GROUP, 2):
-                load_units(x_raw[i], t, value_rows, GROUP * i + t, 2)
             nc.sync.dma_start(
                 out=lw_bf[:, positions, :], in_=logw[positions].rearrange("s b h -> b s h")
             )
@@ -79,13 +82,42 @@ def tile_multiheadattention_pb_kernel(tc, values, logw, Wv, Wo, out):
         load_units(wv_raw, 0, Wv, 0, 1)
         load_units(wv_raw, 1, Wv, 1, 1)
         load_units(wv_raw, 2, Wv, 2, 2)
-        load_group(0)
+        load_pair(0)
+        load_pair(2)
         load_units(wv_raw, 4, Wv, 4, 2)
         load_units(wv_raw, 6, Wv, 6, 2)
-        for i in range(1, N_GROUPS):
-            load_group(i)
-            if i % 2 == 1:
-                load_units(wo_raw, i - 1, Wo, i - 1, 2)
+        load_logw(0)
+        load_pair(4)
+        load_pair(6)
+        load_logw(1)
+        load_pair(8)
+        load_pair(10)
+        load_logw(2)
+        load_units(wo_raw, 0, Wo, 0, 2)
+        load_pair(12)
+        load_pair(14)
+        load_logw(3)
+        load_pair(16)
+        load_pair(18)
+        load_logw(4)
+        load_units(wo_raw, 2, Wo, 2, 2)
+        load_pair(20)
+        load_pair(22)
+        load_logw(5)
+        load_pair(24)
+        load_pair(26)
+        load_logw(6)
+        load_units(wo_raw, 4, Wo, 4, 2)
+        load_pair(28)
+        load_pair(30)
+        load_logw(7)
+        load_units(wo_raw, 6, Wo, 6, 2)
+
+        def raw_unit(s):
+            return x_raw[s // GROUP][:, s % GROUP * DM : (s % GROUP + 1) * DM]
+
+        def w_unit(tile, u):
+            return tile[:, u * DM : (u + 1) * DM]
 
         def split_words(copy, raw, split):
             copy(
@@ -93,88 +125,90 @@ def tile_multiheadattention_pb_kernel(tc, values, logw, Wv, Wo, out):
                 in_=raw.bitcast(F32).rearrange("p (w u) -> p u w", u=2),
             )
 
-        def flip_unit(copy, rows, grouped_words, split):
+        def flip(copy, rows, grouped, is_split):
             words = rows.bitcast(F32)
             flipped = banks.tile([P, PASSES, 2, P], F32, tag="bank")
             for g in range(PASSES):
                 for u in range(2):
-                    if split:
-                        first = u * UNIT_WORDS + g * P
-                        these = slice(first, first + P)
+                    if is_split:
+                        these = slice(u * UNIT_WORDS + g * P, u * UNIT_WORDS + (g + 1) * P)
                     else:
                         these = slice(2 * P * g + u, 2 * P * (g + 1), 2)
                     nc.tensor.transpose(flipped[:, g, u, :], words[:, these], ident[:])
-            copy(out=grouped_words, in_=flipped[:].rearrange("p g u r -> p g r u"))
+            copy(
+                out=grouped.bitcast(F32).rearrange("p (g r u) -> p g r u", g=PASSES, u=2),
+                in_=flipped[:].rearrange("p g u r -> p g r u"),
+            )
 
         def quantise(grouped, codes, scales):
             nc.vector.quantize_mx(out=codes.bitcast(FP8X4), scales=scales, in_=grouped)
 
-        on_vector, on_scalar = nc.vector.tensor_copy, nc.scalar.copy
+        x_split, x_grouped, wv_split, wv_grouped, wo_grouped, vps = {}, {}, {}, {}, {}, {}
 
-        def raw_pair(s):
-            first = s % GROUP * DM
-            return x_raw[s // GROUP][:, first : first + 2 * DM]
+        def split_x(s, copy):
+            if copy is None:
+                return
+            if s // 2 not in x_split:
+                x_split[s // 2] = stage.tile([P, 2 * DM], BF16, tag="x_split", name="x_split")
+            split_words(copy, raw_unit(s), x_split[s // 2][:, s % 2 * DM : (s % 2 + 1) * DM])
+            x_split[s, "done"] = True
 
-        def split_pair(s, copies):
-            split = stage.tile([P, 2 * DM], BF16, tag="x_split", bufs=4)
-            parts = []
-            for t in range(2):
-                cols = slice(t * DM, (t + 1) * DM)
-                if copies[t] is None:
-                    parts.append((raw_pair(s)[:, cols], False))
-                else:
-                    split_words(copies[t], raw_pair(s)[:, cols], split[:, cols])
-                    parts.append((split[:, cols], True))
-            return parts
+        def flip_x(s, copy):
+            if s // 2 not in x_grouped:
+                x_grouped[s // 2] = stage.tile([P, 2 * 4 * UNIT_WORDS], BF16, tag="x_grouped", align_bytes=64, name="x_grouped")
+            grouped = x_grouped[s // 2][:, s % 2 * 4 * UNIT_WORDS : (s % 2 + 1) * 4 * UNIT_WORDS]
+            if (s, "done") in x_split:
+                flip(copy, x_split[s // 2][:, s % 2 * DM : (s % 2 + 1) * DM], grouped, True)
+            else:
+                flip(copy, raw_unit(s), grouped, False)
 
-        def flip_pair(parts, copies, split=None):
-            grouped = stage.tile([P, 2 * 4 * UNIT_WORDS], BF16, tag="x_grouped", bufs=4, align_bytes=64)
-            words = grouped[:].bitcast(F32).rearrange("p (t g r u) -> p t g r u", t=2, g=PASSES, u=2)
-            for t in range(2):
-                flip_unit(copies[t], parts[t][0], words[:, t], parts[t][1])
-            return grouped
+        def quantise_x(s, n):
+            cols = slice(s * UNIT_WORDS, (s + n) * UNIT_WORDS)
+            grouped = x_grouped[s // 2][:, s % 2 * 4 * UNIT_WORDS : (s % 2 + n) * 4 * UNIT_WORDS]
+            quantise(grouped, val_codes[:, cols], val_scales[:, cols])
 
-        def weights_as_floats(i):
+        def logw_as_floats(i):
             positions = slice(GROUP * i, GROUP * (i + 1))
-            nc.scalar.copy(out=lw[:, positions, :], in_=lw_bf[:, positions, :])
+            S(out=lw[:, positions, :], in_=lw_bf[:, positions, :])
 
-        def quantise_pair(grouped, s):
-            cols = slice(s * UNIT_WORDS, (s + 2) * UNIT_WORDS)
-            quantise(grouped[:], val_codes[:, cols], val_scales[:, cols])
+        def split_wv(u, copy):
+            wv_split[u] = stage.tile([P, DM], BF16, tag="w_split", name="w_split")
+            split_words(copy, w_unit(wv_raw, u), wv_split[u][:])
 
-        def split_weight_unit(raw, unit, copy):
-            split = stage.tile([P, DM], BF16, tag="w_split", bufs=4)
-            split_words(copy, raw[:, unit * DM : (unit + 1) * DM], split[:])
-            return split
+        def flip_wv(u, copy):
+            wv_grouped[u] = stage.tile([P, 4 * UNIT_WORDS], BF16, tag="w_grouped", bufs=6, align_bytes=64, name="w_grouped")
+            if u in wv_split:
+                flip(copy, wv_split[u][:], wv_grouped[u][:], True)
+            else:
+                flip(copy, w_unit(wv_raw, u), wv_grouped[u][:], False)
 
-        def flip_split_weight_unit(split, copy):
-            grouped = stage.tile([P, 4 * UNIT_WORDS], BF16, tag="w_grouped", bufs=6, align_bytes=64)
-            words = grouped[:].bitcast(F32).rearrange("p (g r u) -> p g r u", g=PASSES, u=2)
-            flip_unit(copy, split, words, True)
-            return grouped
+        def split_wo(u, copy):
+            split_words(copy, w_unit(wo_raw, u), w_unit(wv_raw, u))
+            wo_grouped[u, "done"] = True
 
-        def flip_weight_unit(raw, unit, copy):
-            grouped = stage.tile([P, 4 * UNIT_WORDS], BF16, tag="w_grouped", bufs=6, align_bytes=64)
-            words = grouped[:].bitcast(F32).rearrange("p (g r u) -> p g r u", g=PASSES, u=2)
-            flip_unit(copy, raw[:, unit * DM : (unit + 1) * DM], words, False)
-            return grouped
+        def flip_wo(u, copy):
+            done = (u, "done") in wo_grouped
+            wo_grouped[u] = stage.tile([P, 4 * UNIT_WORDS], BF16, tag="w_grouped", bufs=6, align_bytes=64, name="w_grouped")
+            flip(copy, w_unit(wv_raw if done else wo_raw, u), wo_grouped[u][:], done)
 
-        def quantise_weight_unit(grouped, codes, scales, unit):
+        def quantise_w(grouped, codes, scales, u):
             for g in range(PASSES):
-                first = g * DP + unit * P
-                quantise(
-                    grouped[:, g * 4 * P : (g + 1) * 4 * P],
-                    codes[:, first : first + P],
-                    scales[:, first : first + P],
-                )
+                cols = slice(g * DP + u * P, g * DP + (u + 1) * P)
+                quantise(grouped[:, g * 4 * P : (g + 1) * 4 * P], codes[:, cols], scales[:, cols])
+
+        def quantise_wv(u):
+            quantise_w(wv_grouped[u], wv_codes, wv_scales, u)
+
+        def quantise_wo(u):
+            quantise_w(wo_grouped[u], wo_codes, wo_scales, u)
 
         def project(s, half):
-            vp = banks.tile([P, N_TILE], F32, tag="bank")
+            vps[s, half] = banks.tile([P, N_TILE], F32, tag="bank", name="vp")
             for g in range(PASSES):
                 rows = slice((s * PASSES + g) * P, (s * PASSES + g + 1) * P)
                 cols = slice(g * DP + half * N_TILE, g * DP + (half + 1) * N_TILE)
                 nc.tensor.matmul_mx(
-                    out=vp[:],
+                    out=vps[s, half][:],
                     lhsT=val_codes[:, rows].bitcast(FP8X4),
                     lhsT_scale=val_scales[:, rows],
                     rhs=wv_codes[:, cols].bitcast(FP8X4),
@@ -182,9 +216,10 @@ def tile_multiheadattention_pb_kernel(tc, values, logw, Wv, Wo, out):
                     start=(g == 0),
                     stop=(g == PASSES - 1),
                 )
-            return vp
 
-        def pool_heads(vp, s, half, on_the_side):
+        def pool(s, half, on_the_side=False):
+            vp = vps[s, half]
+            target = attn if (s, half) == (SL - 1, 1) else acc
             if on_the_side:
                 weighted = stage.tile([P, N_TILE], F32, tag="weighted", bufs=3)
             for j in range(HEADS_PER_HALF):
@@ -197,7 +232,7 @@ def tile_multiheadattention_pb_kernel(tc, values, logw, Wv, Wo, out):
                     )
                 else:
                     nc.vector.scalar_tensor_tensor(
-                        out=acc[:, channels],
+                        out=target[:, channels],
                         in0=vp[:, bank_cols],
                         scalar=lw[:, s, h : h + 1],
                         in1=acc[:, channels],
@@ -208,194 +243,33 @@ def tile_multiheadattention_pb_kernel(tc, values, logw, Wv, Wo, out):
                 side = acc_side[:, half * N_TILE : (half + 1) * N_TILE]
                 w = N_TILE // 2
                 for c in range(0, N_TILE, w):
-                    nc.gpsimd.tensor_tensor(out=side[:, c : c + w], in0=side[:, c : c + w], in1=weighted[:, c : c + w], op=ADD)
+                    piece = slice(c, c + w)
+                    nc.gpsimd.tensor_tensor(out=side[:, piece], in0=side[:, piece], in1=weighted[:, piece], op=ADD)
 
-        def join_sums(half):
+        def join_sums(half, out):
             cols = slice(half * N_TILE, (half + 1) * N_TILE)
-            nc.gpsimd.tensor_tensor(out=acc[:, cols], in0=acc[:, cols], in1=acc_side[:, cols], op=ADD)
-
-        fours = acc[:].rearrange("b (w t) -> b t w", t=4)
+            nc.gpsimd.tensor_tensor(out=out[:, cols], in0=acc[:, cols], in1=acc_side[:, cols], op=ADD)
 
         def warm_up(n):
             for repeat in range(n):
                 scratch = banks.tile([P, N_TILE], F32, tag="bank")
                 nc.tensor.matmul(out=scratch[:], lhsT=zeros[:, 0:P], rhs=zeros[:], start=True, stop=True)
 
-        def flip_attn(g):
-            flipped = banks.tile([P, 4, P], F32, tag="bank")
-            for t in range(4):
-                nc.tensor.transpose(flipped[:, t, :], fours[:, t, g * P : (g + 1) * P], ident[:])
-            grouped = attn_grouped[:, g * 4 * P : (g + 1) * 4 * P]
-            nc.scalar.copy(
-                out=grouped.rearrange("p (b t) -> p b t", t=4),
-                in_=flipped[:].rearrange("p t b -> p b t"),
+        def flip_attn(g, copy):
+            words = attn[:].bitcast(F32)
+            flipped = banks.tile([P, 2, P], F32, tag="bank")
+            for u in range(2):
+                nc.tensor.transpose(flipped[:, u, :], words[:, 2 * P * g + u : 2 * P * (g + 1) : 2], ident[:])
+            copy(
+                out=attn_grouped[:, g * 4 * P : (g + 1) * 4 * P].bitcast(F32).rearrange("p (b u) -> p b u", u=2),
+                in_=flipped[:].rearrange("p u b -> p b u"),
             )
-            quantise(grouped, attn_codes[:, g * P : (g + 1) * P], attn_scales[:, g * P : (g + 1) * P])
 
-        V, S = nc.vector.tensor_copy, nc.scalar.copy
-
-        def split_group(i, copies):
-            return [split_pair(4 * i, copies[0:2]), split_pair(4 * i + 2, copies[2:4])]
-
-        def flip_group(parts, copies):
-            return [flip_pair(parts[0], copies[0:2]), flip_pair(parts[1], copies[2:4])]
-
-        def flip_weights(units, copies):
-            return [(unit, flip_weight_unit(wo_raw, unit, copies[n])) for n, unit in enumerate(units)]
-
-        w_split, w_grp, x_split_t, x_grp = {}, {}, {}, {}
-
-        def quantise_position(s):
-            cols = slice(s * UNIT_WORDS, (s + 1) * UNIT_WORDS)
-            grouped = x_grp[s // 2][:, s % 2 * 4 * UNIT_WORDS : (s % 2 + 1) * 4 * UNIT_WORDS]
-            quantise(grouped, val_codes[:, cols], val_scales[:, cols])
-
-        def flip_position(s, copy):
-            if s % 2 == 0:
-                x_grp[s // 2] = stage.tile([P, 2 * 4 * UNIT_WORDS], BF16, tag="x_grouped", bufs=4, align_bytes=64, name="x_grouped")
-            words = x_grp[s // 2][:].bitcast(F32).rearrange("p (t g r u) -> p t g r u", t=2, g=PASSES, u=2)
-            raw = raw_pair(s // 2 * 2)[:, s % 2 * DM : (s % 2 + 1) * DM]
-            if s in x_split_t:
-                flip_unit(copy, x_split_t[s], words[:, s % 2], True)
-            else:
-                flip_unit(copy, raw, words[:, s % 2], False)
-
-        def split_position(s, copy):
-            if s % 2 == 0:
-                x_split_t["pair"] = stage.tile([P, 2 * DM], BF16, tag="x_split", bufs=4, name="x_split")
-            part = x_split_t["pair"][:, s % 2 * DM : (s % 2 + 1) * DM]
-            split_words(copy, raw_pair(s // 2 * 2)[:, s % 2 * DM : (s % 2 + 1) * DM], part)
-            x_split_t[s] = part
-
-        def flip_w(u, copy):
-            if u in w_split:
-                w_grp[u] = flip_split_weight_unit(w_split[u][:], copy)
-            else:
-                w_grp[u] = flip_weight_unit(wv_raw, u, copy)
-
-        def bank(s, half):
-            pool_heads(project(s, half), s, half, False)
-
-        vps = {}
-        warm_up(5)
-        w_split[0] = split_weight_unit(wv_raw, 0, V)
-        flip_w(0, S)
-        w_split[1] = split_weight_unit(wv_raw, 1, V)
-        warm_up(1)
-        flip_w(1, S)
-        w_split[2] = split_weight_unit(wv_raw, 2, V)
-        warm_up(1)
-        quantise_weight_unit(w_grp[0], wv_codes, wv_scales, 0)
-        flip_w(2, S)
-        w_split[3] = split_weight_unit(wv_raw, 3, V)
-        quantise_weight_unit(w_grp[1], wv_codes, wv_scales, 1)
-        flip_w(3, S)
-        warm_up(1)
-        split_position(0, V)
-        quantise_weight_unit(w_grp[2], wv_codes, wv_scales, 2)
-        flip_position(0, S)
-        split_position(1, V)
-        warm_up(1)
-        flip_position(1, S)
-        split_position(2, V)
-        warm_up(1)
-        flip_position(2, S)
-        split_position(3, V)
-        quantise_weight_unit(w_grp[3], wv_codes, wv_scales, 3)
-        flip_position(3, S)
-        quantise_position(0)
-        weights_as_floats(0)
-        w_split[4] = split_weight_unit(wv_raw, 4, V)
-        quantise_position(1)
-        w_split[5] = split_weight_unit(wv_raw, 5, V)
-        vps[0, 0] = project(0, 0)
-        vps[1, 0] = project(1, 0)
-        quantise_position(2)
-        w_split[6] = split_weight_unit(wv_raw, 6, V)
-        quantise_position(3)
-        w_split[7] = split_weight_unit(wv_raw, 7, V)
-        split_position(4, S)
-        split_position(5, S)
-        flip_w(4, S)
-        flip_w(5, S)
-        flip_w(6, S)
-        flip_w(7, S)
-        pool_heads(vps[0, 0], 0, 0, False)
-        pool_heads(vps[1, 0], 1, 0, False)
-        vps[2, 0] = project(2, 0)
-        vps[3, 0] = project(3, 0)
-        quantise_weight_unit(w_grp[4], wv_codes, wv_scales, 4)
-        pool_heads(vps[2, 0], 2, 0, False)
-        quantise_weight_unit(w_grp[5], wv_codes, wv_scales, 5)
-        pool_heads(vps[3, 0], 3, 0, False)
-        flip_position(4, S)
-        flip_position(5, S)
-        flip_position(6, S)
-        flip_position(7, S)
-        warm_up(2)
-        quantise_weight_unit(w_grp[6], wv_codes, wv_scales, 6)
-        quantise_weight_unit(w_grp[7], wv_codes, wv_scales, 7)
-        weights_as_floats(1)
-        x_split = split_group(2, (V, V, V, V))
-        vps[0, 1] = project(0, 1)
-        pool_heads(vps[0, 1], 0, 1, False)
-        vps[1, 1] = project(1, 1)
-        quantise_pair(x_grp[4 // 2], 4)
-        pool_heads(vps[1, 1], 1, 1, False)
-        vps[2, 1] = project(2, 1)
-        quantise_pair(x_grp[6 // 2], 6)
-        pool_heads(vps[2, 1], 2, 1, False)
-        vps[3, 1] = project(3, 1)
-        pool_heads(vps[3, 1], 3, 1, False)
-        sides = {}
-        wo_runs = [(4, 4, (0,1,2,3,)), (5, 4, (4,5,6,7,))]
-        wo_splits = [(1, 5, (0,)), (1, 7, (1,)), (2, 5, (2,)), (2, 7, (3,)), (3, 5, (4,)), (3, 7, (5,)), (4, 5, (6,)), (4, 7, (7,))]
-        wo_quants = [(5, 0, (0,1,2,3,)), (6, 0, (4,5,6,7,))]
-        wd = (S,S,S,S)
-        wc = (S,S,S,S)
-        wo_split = {}
-        wo_grouped = {}
-
-        def wo_events(i, n):
-            for r, m, units in wo_splits:
-                if (r, m) == (i, n):
-                    for u in units:
-                        wo_split[u] = wv_raw[:, u * DM : (u + 1) * DM]
-                        split_words(wd[u % 4], wo_raw[:, u * DM : (u + 1) * DM], wo_split[u])
-            for r, m, units in wo_runs:
-                if (r, m) == (i, n):
-                    for u in units:
-                        wo_grouped[u] = flip_split_weight_unit(wo_split[u], wc[u % 4])
-            for r, m, units in wo_quants:
-                if (r, m) == (i, n):
-                    for u in units:
-                        quantise_weight_unit(wo_grouped[u], wo_codes, wo_scales, u)
-
-        x_now = flip_group(x_split, (S, S, S, S))
-        for i in range(1, 8):
-            order = [(4 * i + t, half) for t in range(4) for half in range(2)]
-            if i == 7:
-                order = [(4 * i + t, half) for half in range(2) for t in range(4)]
-            side = (0,) if i == 7 else (0,2,4,) if i == 6 else sides.get(i, (2,))
-            for n, (s, half) in enumerate(order):
-                wo_events(i, n)
-                if i < 7:
-                    if n == 0:
-                        quantise_pair(x_now[0], 4 * i + 4)
-                    if n == 1:
-                        quantise_pair(x_now[1], 4 * i + 6)
-                        weights_as_floats(i + 1)
-                pool_heads(project(s, half), s, half, n in side)
-                if n == 1 and i + 2 < 8:
-                    x_split = split_group(i + 2, (S, S, S, S))
-                if i == 7 and n == 5:
-                    join_sums(0)
-            if i + 2 < 8:
-                x_now = flip_group(x_split, (S, S, S, S))
-            wo_events(i, 8)
+        def quantise_attn(g):
+            cols = slice(g * P, (g + 1) * P)
+            quantise(attn_grouped[:, g * 4 * P : (g + 1) * 4 * P], attn_codes[:, cols], attn_scales[:, cols])
 
         quarter = DO // 4
-        out_sums = [banks.tile([P, quarter], F32, tag="bank", name="out_sums%d" % n) for n in range(4)]
 
         def project_out(g):
             for n in range(4):
@@ -410,10 +284,282 @@ def tile_multiheadattention_pb_kernel(tc, values, logw, Wv, Wo, out):
                     stop=(g == PASSES - 1),
                 )
 
-        flip_attn(0)
-        flip_attn(1)
+        warm_up(5)
+        flip_wv(0, S)
+        warm_up(1)
+        flip_wv(1, S)
+        warm_up(1)
+        quantise_wv(0)
+        flip_wv(2, S)
+        quantise_wv(1)
+        flip_wv(3, S)
+        warm_up(1)
+        split_x(0, V)
+        quantise_wv(2)
+        flip_x(0, S)
+        split_x(1, V)
+        warm_up(1)
+        flip_x(1, S)
+        split_x(2, V)
+        warm_up(1)
+        flip_x(2, S)
+        split_x(3, V)
+        quantise_wv(3)
+        flip_x(3, S)
+        quantise_x(0, 1)
+        logw_as_floats(0)
+        split_wv(4, V)
+        quantise_x(1, 1)
+        split_wv(5, V)
+        project(0, 0)
+        project(1, 0)
+        quantise_x(2, 1)
+        split_wv(6, V)
+        quantise_x(3, 1)
+        split_wv(7, V)
+        split_x(4, S)
+        split_x(5, S)
+        flip_wv(4, S)
+        flip_wv(5, S)
+        flip_wv(6, S)
+        flip_wv(7, S)
+        pool(0, 0)
+        pool(1, 0)
+        project(2, 0)
+        project(3, 0)
+        quantise_wv(4)
+        pool(2, 0)
+        quantise_wv(5)
+        pool(3, 0)
+        flip_x(4, S)
+        flip_x(5, S)
+        flip_x(6, S)
+        flip_x(7, S)
+        warm_up(2)
+        quantise_wv(6)
+        quantise_wv(7)
+        logw_as_floats(1)
+        split_x(8, V)
+        split_x(9, V)
+        split_x(10, V)
+        split_x(11, V)
+        project(0, 1)
+        pool(0, 1)
+        project(1, 1)
+        quantise_x(4, 2)
+        pool(1, 1)
+        project(2, 1)
+        quantise_x(6, 2)
+        pool(2, 1)
+        project(3, 1)
+        pool(3, 1)
+        flip_x(8, S)
+        flip_x(9, S)
+        flip_x(10, S)
+        flip_x(11, S)
+        quantise_x(8, 2)
+        project(4, 0)
+        pool(4, 0, True)
+        quantise_x(10, 2)
+        logw_as_floats(2)
+        project(4, 1)
+        pool(4, 1)
+        split_x(12, V)
+        split_x(13, S)
+        split_x(14, V)
+        split_x(15, S)
+        project(5, 0)
+        pool(5, 0)
+        project(5, 1)
+        pool(5, 1)
+        project(6, 0)
+        pool(6, 0, True)
+        split_wo(0, S)
+        project(6, 1)
+        pool(6, 1)
+        project(7, 0)
+        pool(7, 0)
+        split_wo(1, S)
+        project(7, 1)
+        pool(7, 1)
+        flip_x(12, S)
+        flip_x(13, S)
+        flip_x(14, S)
+        flip_x(15, S)
+        quantise_x(12, 2)
+        project(8, 0)
+        pool(8, 0, True)
+        quantise_x(14, 2)
+        logw_as_floats(3)
+        project(8, 1)
+        pool(8, 1)
+        split_x(16, V)
+        split_x(17, S)
+        split_x(18, V)
+        split_x(19, S)
+        project(9, 0)
+        pool(9, 0)
+        project(9, 1)
+        pool(9, 1)
+        project(10, 0)
+        pool(10, 0, True)
+        split_wo(2, S)
+        project(10, 1)
+        pool(10, 1)
+        project(11, 0)
+        pool(11, 0)
+        split_wo(3, S)
+        project(11, 1)
+        pool(11, 1)
+        flip_x(16, S)
+        flip_x(17, S)
+        flip_x(18, S)
+        flip_x(19, S)
+        quantise_x(16, 2)
+        project(12, 0)
+        pool(12, 0, True)
+        quantise_x(18, 2)
+        logw_as_floats(4)
+        project(12, 1)
+        pool(12, 1)
+        split_x(20, V)
+        split_x(21, S)
+        split_x(22, V)
+        split_x(23, S)
+        project(13, 0)
+        pool(13, 0)
+        project(13, 1)
+        pool(13, 1)
+        project(14, 0)
+        pool(14, 0, True)
+        split_wo(4, S)
+        project(14, 1)
+        pool(14, 1)
+        project(15, 0)
+        pool(15, 0)
+        split_wo(5, S)
+        project(15, 1)
+        pool(15, 1)
+        flip_x(20, S)
+        flip_x(21, S)
+        flip_x(22, S)
+        flip_x(23, S)
+        quantise_x(20, 2)
+        project(16, 0)
+        pool(16, 0, True)
+        quantise_x(22, 2)
+        logw_as_floats(5)
+        project(16, 1)
+        pool(16, 1)
+        split_x(24, V)
+        split_x(25, S)
+        split_x(26, V)
+        split_x(27, S)
+        project(17, 0)
+        pool(17, 0)
+        project(17, 1)
+        pool(17, 1)
+        flip_wo(0, S)
+        flip_wo(1, S)
+        flip_wo(2, S)
+        flip_wo(3, S)
+        project(18, 0)
+        pool(18, 0, True)
+        split_wo(6, S)
+        project(18, 1)
+        pool(18, 1)
+        project(19, 0)
+        pool(19, 0)
+        split_wo(7, S)
+        project(19, 1)
+        pool(19, 1)
+        flip_x(24, S)
+        flip_x(25, S)
+        flip_x(26, S)
+        flip_x(27, S)
+        quantise_wo(0)
+        quantise_wo(1)
+        quantise_wo(2)
+        quantise_wo(3)
+        quantise_x(24, 2)
+        project(20, 0)
+        pool(20, 0, True)
+        quantise_x(26, 2)
+        logw_as_floats(6)
+        project(20, 1)
+        pool(20, 1)
+        split_x(28, V)
+        split_x(29, S)
+        split_x(30, V)
+        split_x(31, S)
+        project(21, 0)
+        pool(21, 0)
+        project(21, 1)
+        pool(21, 1)
+        flip_wo(4, S)
+        flip_wo(5, S)
+        flip_wo(6, S)
+        flip_wo(7, S)
+        project(22, 0)
+        pool(22, 0, True)
+        project(22, 1)
+        pool(22, 1)
+        project(23, 0)
+        pool(23, 0)
+        project(23, 1)
+        pool(23, 1)
+        flip_x(28, S)
+        flip_x(29, S)
+        flip_x(30, S)
+        flip_x(31, S)
+        quantise_wo(4)
+        quantise_wo(5)
+        quantise_wo(6)
+        quantise_wo(7)
+        quantise_x(28, 2)
+        project(24, 0)
+        pool(24, 0, True)
+        quantise_x(30, 2)
+        logw_as_floats(7)
+        project(24, 1)
+        pool(24, 1)
+        project(25, 0)
+        pool(25, 0, True)
+        project(25, 1)
+        pool(25, 1)
+        project(26, 0)
+        pool(26, 0, True)
+        project(26, 1)
+        pool(26, 1)
+        project(27, 0)
+        pool(27, 0)
+        project(27, 1)
+        pool(27, 1)
+        project(28, 0)
+        pool(28, 0, True)
+        project(29, 0)
+        pool(29, 0)
+        project(30, 0)
+        pool(30, 0, True)
+        project(31, 0)
+        pool(31, 0)
+        project(28, 1)
+        pool(28, 1)
+        join_sums(0, attn)
+        project(29, 1)
+        pool(29, 1)
+        project(30, 1)
+        pool(30, 1)
+        project(31, 1)
+        pool(31, 1)
+        out_sums = [banks.tile([P, quarter], F32, tag="bank", name="out_sums%d" % n) for n in range(4)]
+        flip_attn(0, S)
+        quantise_attn(0)
+        flip_attn(1, V)
+        quantise_attn(1)
         project_out(0)
         project_out(1)
+
         for n in range(4):
             cols = slice(n * quarter, (n + 1) * quarter)
             (S, V)[n % 2](out=out_sb[:, cols], in_=out_sums[n][:])

@@ -241,7 +241,7 @@ def tile_multiheadattention_pb_kernel(tc, values, logw, Wv, Wo, out):
                     )
             if on_the_side:
                 side = acc_side[:, half * N_TILE : (half + 1) * N_TILE]
-                w = N_TILE // 2
+                w = N_TILE // 1
                 for c in range(0, N_TILE, w):
                     piece = slice(c, c + w)
                     nc.gpsimd.tensor_tensor(out=side[:, piece], in0=side[:, piece], in1=weighted[:, piece], op=ADD)
@@ -285,25 +285,25 @@ def tile_multiheadattention_pb_kernel(tc, values, logw, Wv, Wo, out):
                 )
 
         warm_up(5)
+        split_wv(0, V)
         flip_wv(0, S)
+        split_wv(1, V)
         warm_up(1)
         flip_wv(1, S)
+        split_wv(2, V)
         warm_up(1)
         quantise_wv(0)
         flip_wv(2, S)
+        split_wv(3, V)
         quantise_wv(1)
         flip_wv(3, S)
         warm_up(1)
-        split_x(0, V)
         quantise_wv(2)
         flip_x(0, S)
-        split_x(1, V)
         warm_up(1)
         flip_x(1, S)
-        split_x(2, V)
         warm_up(1)
         flip_x(2, S)
-        split_x(3, V)
         quantise_wv(3)
         flip_x(3, S)
         quantise_x(0, 1)
@@ -359,21 +359,20 @@ def tile_multiheadattention_pb_kernel(tc, values, logw, Wv, Wo, out):
         flip_x(11, S)
         quantise_x(8, 2)
         project(4, 0)
-        pool(4, 0, True)
+        pool(4, 0)
         quantise_x(10, 2)
         logw_as_floats(2)
         project(4, 1)
         pool(4, 1)
-        split_x(12, V)
+        split_x(12, S)
         split_x(13, S)
-        split_x(14, V)
-        split_x(15, S)
+        split_x(14, S)
         project(5, 0)
-        pool(5, 0)
+        pool(5, 0, True)
         project(5, 1)
         pool(5, 1)
         project(6, 0)
-        pool(6, 0, True)
+        pool(6, 0)
         split_wo(0, S)
         project(6, 1)
         pool(6, 1)
@@ -388,21 +387,20 @@ def tile_multiheadattention_pb_kernel(tc, values, logw, Wv, Wo, out):
         flip_x(15, S)
         quantise_x(12, 2)
         project(8, 0)
-        pool(8, 0, True)
+        pool(8, 0)
         quantise_x(14, 2)
         logw_as_floats(3)
         project(8, 1)
         pool(8, 1)
-        split_x(16, V)
+        split_x(16, S)
         split_x(17, S)
-        split_x(18, V)
-        split_x(19, S)
+        split_x(18, S)
         project(9, 0)
-        pool(9, 0)
+        pool(9, 0, True)
         project(9, 1)
         pool(9, 1)
         project(10, 0)
-        pool(10, 0, True)
+        pool(10, 0)
         split_wo(2, S)
         project(10, 1)
         pool(10, 1)
@@ -417,21 +415,20 @@ def tile_multiheadattention_pb_kernel(tc, values, logw, Wv, Wo, out):
         flip_x(19, S)
         quantise_x(16, 2)
         project(12, 0)
-        pool(12, 0, True)
+        pool(12, 0)
         quantise_x(18, 2)
         logw_as_floats(4)
         project(12, 1)
         pool(12, 1)
-        split_x(20, V)
+        split_x(20, S)
         split_x(21, S)
-        split_x(22, V)
-        split_x(23, S)
+        split_x(22, S)
         project(13, 0)
-        pool(13, 0)
+        pool(13, 0, True)
         project(13, 1)
         pool(13, 1)
         project(14, 0)
-        pool(14, 0, True)
+        pool(14, 0)
         split_wo(4, S)
         project(14, 1)
         pool(14, 1)
@@ -446,17 +443,16 @@ def tile_multiheadattention_pb_kernel(tc, values, logw, Wv, Wo, out):
         flip_x(23, S)
         quantise_x(20, 2)
         project(16, 0)
-        pool(16, 0, True)
+        pool(16, 0)
         quantise_x(22, 2)
         logw_as_floats(5)
         project(16, 1)
         pool(16, 1)
-        split_x(24, V)
+        split_x(24, S)
         split_x(25, S)
-        split_x(26, V)
-        split_x(27, S)
+        split_x(26, S)
         project(17, 0)
-        pool(17, 0)
+        pool(17, 0, True)
         project(17, 1)
         pool(17, 1)
         flip_wo(0, S)
@@ -464,7 +460,7 @@ def tile_multiheadattention_pb_kernel(tc, values, logw, Wv, Wo, out):
         flip_wo(2, S)
         flip_wo(3, S)
         project(18, 0)
-        pool(18, 0, True)
+        pool(18, 0)
         split_wo(6, S)
         project(18, 1)
         pool(18, 1)
@@ -483,17 +479,16 @@ def tile_multiheadattention_pb_kernel(tc, values, logw, Wv, Wo, out):
         quantise_wo(3)
         quantise_x(24, 2)
         project(20, 0)
-        pool(20, 0, True)
+        pool(20, 0)
         quantise_x(26, 2)
         logw_as_floats(6)
         project(20, 1)
         pool(20, 1)
-        split_x(28, V)
+        split_x(28, S)
         split_x(29, S)
-        split_x(30, V)
-        split_x(31, S)
+        split_x(30, S)
         project(21, 0)
-        pool(21, 0)
+        pool(21, 0, True)
         project(21, 1)
         pool(21, 1)
         flip_wo(4, S)
@@ -501,7 +496,7 @@ def tile_multiheadattention_pb_kernel(tc, values, logw, Wv, Wo, out):
         flip_wo(6, S)
         flip_wo(7, S)
         project(22, 0)
-        pool(22, 0, True)
+        pool(22, 0)
         project(22, 1)
         pool(22, 1)
         project(23, 0)
@@ -540,7 +535,7 @@ def tile_multiheadattention_pb_kernel(tc, values, logw, Wv, Wo, out):
         project(29, 0)
         pool(29, 0)
         project(30, 0)
-        pool(30, 0, True)
+        pool(30, 0)
         project(31, 0)
         pool(31, 0)
         project(28, 1)

@@ -81,14 +81,21 @@ def tile_multiheadattention_pb_kernel(tc, values, logw, Wv, Wo, out):
 
         load_units(wv_raw, 0, Wv, 0, 1)
         load_units(wv_raw, 1, Wv, 1, 1)
-        load_units(wv_raw, 2, Wv, 2, 2)
-        load_pair(0)
-        load_pair(2)
-        load_units(wv_raw, 4, Wv, 4, 2)
-        load_units(wv_raw, 6, Wv, 6, 2)
+        load_units(wv_raw, 2, Wv, 2, 1)
+        load_units(wv_raw, 3, Wv, 3, 1)
+        load_units(x_raw[0], 0, value_rows, 0, 1)
+        load_units(x_raw[0], 1, value_rows, 1, 1)
+        load_units(x_raw[0], 2, value_rows, 2, 1)
+        load_units(x_raw[0], 3, value_rows, 3, 1)
+        load_units(wv_raw, 4, Wv, 4, 1)
+        load_units(wv_raw, 5, Wv, 5, 1)
+        load_units(wv_raw, 6, Wv, 6, 1)
+        load_units(wv_raw, 7, Wv, 7, 1)
         load_logw(0)
-        load_pair(4)
-        load_pair(6)
+        load_units(x_raw[1], 0, value_rows, 4, 1)
+        load_units(x_raw[1], 1, value_rows, 5, 1)
+        load_units(x_raw[1], 2, value_rows, 6, 1)
+        load_units(x_raw[1], 3, value_rows, 7, 1)
         load_logw(1)
         load_pair(8)
         load_pair(10)
@@ -298,12 +305,16 @@ def tile_multiheadattention_pb_kernel(tc, values, logw, Wv, Wo, out):
         quantise_wv(1)
         flip_wv(3, S)
         warm_up(1)
+        split_x(0, V)
         quantise_wv(2)
         flip_x(0, S)
+        split_x(1, V)
         warm_up(1)
         flip_x(1, S)
+        split_x(2, V)
         warm_up(1)
         flip_x(2, S)
+        split_x(3, V)
         quantise_wv(3)
         flip_x(3, S)
         quantise_x(0, 1)
@@ -335,7 +346,7 @@ def tile_multiheadattention_pb_kernel(tc, values, logw, Wv, Wo, out):
         flip_x(5, S)
         flip_x(6, S)
         flip_x(7, S)
-        warm_up(2)
+        warm_up(1)
         quantise_wv(6)
         quantise_wv(7)
         logw_as_floats(1)

@@ -91,8 +91,8 @@ def tile_multiheadattention_pb_kernel(tc, values, logw, Wv, Wo, out):
         load_units(wv_raw, 5, Wv, 5, 1)
         load_units(wv_raw, 6, Wv, 6, 1)
         load_units(wv_raw, 7, Wv, 7, 1)
-        load_logw(0)
         load_units(x_raw[1], 0, value_rows, 4, 1)
+        load_logw(0)
         load_units(x_raw[1], 1, value_rows, 5, 1)
         load_units(x_raw[1], 2, value_rows, 6, 1)
         load_units(x_raw[1], 3, value_rows, 7, 1)
@@ -241,7 +241,7 @@ def tile_multiheadattention_pb_kernel(tc, values, logw, Wv, Wo, out):
                     nc.vector.scalar_tensor_tensor(
                         out=target[:, channels],
                         in0=vp[:, bank_cols],
-                        scalar=lw[:, s, h : h + 1],
+                        scalar=lw_bf[:, s, h : h + 1],
                         in1=acc[:, channels],
                         op0=MULT,
                         op1=ADD,
@@ -318,7 +318,6 @@ def tile_multiheadattention_pb_kernel(tc, values, logw, Wv, Wo, out):
         quantise_wv(3)
         flip_x(3, S)
         quantise_x(0, 1)
-        logw_as_floats(0)
         split_wv(4, V)
         quantise_x(1, 1)
         split_wv(5, V)
@@ -569,4 +568,4 @@ def tile_multiheadattention_pb_kernel(tc, values, logw, Wv, Wo, out):
         for n in range(4):
             cols = slice(n * quarter, (n + 1) * quarter)
             (S, V)[n % 2](out=out_sb[:, cols], in_=out_sums[n][:])
-            nc.sync.dma_start(out=out[:, cols], in_=out_sb[:, cols])
+            (nc.scalar, nc.sync)[n % 2].dma_start(out=out[:, cols], in_=out_sb[:, cols])

@@ -20,10 +20,12 @@ PASSES = DM // K_PASS
 N_TILE = 512
 HALVES = DP // N_TILE
 HEADS_PER_HALF = N_TILE // HEAD_DIM
-GROUP = 4
-N_GROUPS = SL // GROUP
 W_UNITS = DP // P
 UNIT_WORDS = PASSES * P
+UNIT_GROUPED = 4 * UNIT_WORDS
+ROUND = 4
+N_ROUNDS = SL // ROUND
+OUT_TILE = 256
 
 FLOPS = 2 * SL * P * DM * DP + 2 * P * DP * DO
 
@@ -35,7 +37,6 @@ def tile_multiheadattention_pb_kernel(tc, values, logw, Wv, Wo, out):
         stage = ctx.enter_context(tc.tile_pool(name="stage", bufs=4))
         banks = ctx.enter_context(tc.psum_pool(name="banks", bufs=8))
         ctx.enter_context(tc.manual_schedule())
-        V, S = nc.vector.tensor_copy, nc.scalar.copy
 
         ident = keep.tile([P, P], F32)
         make_identity(nc, ident[:])
@@ -43,92 +44,64 @@ def tile_multiheadattention_pb_kernel(tc, values, logw, Wv, Wo, out):
         nc.vector.memset(zeros[:], 0.0)
         acc = keep.tile([P, DP], F32)
         nc.vector.memset(acc[:], 0.0)
-        acc_side = keep.tile([P, DP], F32)
+        acc_side = keep.tile([P, N_TILE], F32)
         nc.gpsimd.memset(acc_side[:], 0.0)
 
-        x_raw = [keep.tile([P, GROUP * DM], BF16, name="x_raw%d" % i) for i in range(N_GROUPS)]
+        x_raw = keep.tile([P, SL * DM], BF16)
         wv_raw = keep.tile([P, W_UNITS * DM], BF16)
         wo_raw = keep.tile([P, W_UNITS * DM], BF16)
-        lw_bf = keep.tile([P, SL, HEADS], BF16)
-        lw = keep.tile([P, SL, HEADS], F32)
-        val_codes = keep.tile([P, SL * UNIT_WORDS], U32, align_bytes=64)
-        val_scales = keep.tile([P, SL * UNIT_WORDS], U8, align_bytes=64)
+        logw_raw = keep.tile([P, SL, HEADS], BF16)
+        logw_side = keep.tile([P, SL, HEADS], F32)
+        x_codes = keep.tile([P, SL * UNIT_WORDS], U32, align_bytes=64)
+        x_scales = keep.tile([P, SL * UNIT_WORDS], U8, align_bytes=64)
         wv_codes = keep.tile([P, PASSES * DP], U32, align_bytes=64)
         wv_scales = keep.tile([P, PASSES * DP], U8, align_bytes=64)
         wo_codes = keep.tile([P, PASSES * DO], U32, align_bytes=64)
         wo_scales = keep.tile([P, PASSES * DO], U8, align_bytes=64)
         attn = keep.tile([P, DP], BF16)
-        attn_grouped = keep.tile([P, 4 * UNIT_WORDS], BF16, align_bytes=64)
+        attn_grouped = keep.tile([P, UNIT_GROUPED], BF16, align_bytes=64)
         attn_codes = keep.tile([P, UNIT_WORDS], U32, align_bytes=64)
         attn_scales = keep.tile([P, UNIT_WORDS], U8, align_bytes=64)
         out_sb = keep.tile([P, DO], F32)
 
-        def load_units(raw, slot, matrix, unit, n):
+        def load(raw, matrix, unit, n):
             src = matrix[unit * P : (unit + n) * P, :].rearrange("(t p) k -> p t k", p=P)
-            dst = raw[:, slot * DM : (slot + n) * DM].rearrange("p (t k) -> p t k", t=n)
+            dst = raw[:, unit * DM : (unit + n) * DM].rearrange("p (t k) -> p t k", t=n)
             nc.sync.dma_start(out=dst, in_=src)
 
         value_rows = values.flatten_outer_dims()
 
-        def load_pair(s):
-            load_units(x_raw[s // GROUP], s % GROUP, value_rows, s, 2)
-
         def load_logw(i):
-            positions = slice(GROUP * i, GROUP * (i + 1))
+            positions = slice(ROUND * i, ROUND * (i + 1))
             nc.sync.dma_start(
-                out=lw_bf[:, positions, :], in_=logw[positions].rearrange("s b h -> b s h")
+                out=logw_raw[:, positions, :], in_=logw[positions].rearrange("s b h -> b s h")
             )
 
-        load_units(wv_raw, 0, Wv, 0, 1)
-        load_units(wv_raw, 1, Wv, 1, 1)
-        load_units(wv_raw, 2, Wv, 2, 1)
-        load_units(wv_raw, 3, Wv, 3, 1)
-        load_units(x_raw[0], 0, value_rows, 0, 1)
-        load_units(x_raw[0], 1, value_rows, 1, 1)
-        load_units(x_raw[0], 2, value_rows, 2, 1)
-        load_units(x_raw[0], 3, value_rows, 3, 1)
-        load_units(wv_raw, 4, Wv, 4, 1)
-        load_units(wv_raw, 5, Wv, 5, 1)
-        load_units(wv_raw, 6, Wv, 6, 1)
-        load_units(wv_raw, 7, Wv, 7, 1)
-        load_units(x_raw[1], 0, value_rows, 4, 1)
+        for u in range(4):
+            load(wv_raw, Wv, u, 1)
+        for s in range(4):
+            load(x_raw, value_rows, s, 1)
+        for u in range(4, 8):
+            load(wv_raw, Wv, u, 1)
         load_logw(0)
-        load_units(x_raw[1], 1, value_rows, 5, 1)
-        load_units(x_raw[1], 2, value_rows, 6, 1)
-        load_units(x_raw[1], 3, value_rows, 7, 1)
+        for s in range(4, 8):
+            load(x_raw, value_rows, s, 1)
         load_logw(1)
-        load_pair(8)
-        load_pair(10)
-        load_logw(2)
-        load_units(wo_raw, 0, Wo, 0, 2)
-        load_pair(12)
-        load_pair(14)
-        load_logw(3)
-        load_pair(16)
-        load_pair(18)
-        load_logw(4)
-        load_units(wo_raw, 2, Wo, 2, 2)
-        load_pair(20)
-        load_pair(22)
-        load_logw(5)
-        load_pair(24)
-        load_pair(26)
-        load_logw(6)
-        load_units(wo_raw, 4, Wo, 4, 2)
-        load_pair(28)
-        load_pair(30)
-        load_logw(7)
-        load_units(wo_raw, 6, Wo, 6, 2)
+        for i in range(2, N_ROUNDS):
+            load(x_raw, value_rows, ROUND * i, 2)
+            load(x_raw, value_rows, ROUND * i + 2, 2)
+            load_logw(i)
+            if i in (2, 3, 4, 5):
+                load(wo_raw, Wo, 2 * (i - 2), 2)
 
-        def raw_unit(s):
-            return x_raw[s // GROUP][:, s % GROUP * DM : (s % GROUP + 1) * DM]
+        on_vector, on_scalar = nc.vector.tensor_copy, nc.scalar.copy
 
-        def w_unit(tile, u):
+        def unit_of(tile, u):
             return tile[:, u * DM : (u + 1) * DM]
 
-        def split_words(copy, raw, split):
+        def split(copy, raw, halves):
             copy(
-                out=split.bitcast(F32).rearrange("p (u w) -> p u w", u=2),
+                out=halves.bitcast(F32).rearrange("p (u w) -> p u w", u=2),
                 in_=raw.bitcast(F32).rearrange("p (w u) -> p u w", u=2),
             )
 
@@ -138,10 +111,10 @@ def tile_multiheadattention_pb_kernel(tc, values, logw, Wv, Wo, out):
             for g in range(PASSES):
                 for u in range(2):
                     if is_split:
-                        these = slice(u * UNIT_WORDS + g * P, u * UNIT_WORDS + (g + 1) * P)
+                        these = words[:, u * UNIT_WORDS + g * P : u * UNIT_WORDS + (g + 1) * P]
                     else:
-                        these = slice(2 * P * g + u, 2 * P * (g + 1), 2)
-                    nc.tensor.transpose(flipped[:, g, u, :], words[:, these], ident[:])
+                        these = words[:, 2 * P * g + u : 2 * P * (g + 1) : 2]
+                    nc.tensor.transpose(flipped[:, g, u, :], these, ident[:])
             copy(
                 out=grouped.bitcast(F32).rearrange("p (g r u) -> p g r u", g=PASSES, u=2),
                 in_=flipped[:].rearrange("p g u r -> p g r u"),
@@ -150,112 +123,109 @@ def tile_multiheadattention_pb_kernel(tc, values, logw, Wv, Wo, out):
         def quantise(grouped, codes, scales):
             nc.vector.quantize_mx(out=codes.bitcast(FP8X4), scales=scales, in_=grouped)
 
-        x_split, x_grouped, wv_split, wv_grouped, wo_grouped, vps = {}, {}, {}, {}, {}, {}
-
-        def split_x(s, copy):
-            if copy is None:
-                return
-            if s // 2 not in x_split:
-                x_split[s // 2] = stage.tile([P, 2 * DM], BF16, tag="x_split", name="x_split")
-            split_words(copy, raw_unit(s), x_split[s // 2][:, s % 2 * DM : (s % 2 + 1) * DM])
-            x_split[s, "done"] = True
-
-        def flip_x(s, copy):
-            if s // 2 not in x_grouped:
-                x_grouped[s // 2] = stage.tile([P, 2 * 4 * UNIT_WORDS], BF16, tag="x_grouped", align_bytes=64, name="x_grouped")
-            grouped = x_grouped[s // 2][:, s % 2 * 4 * UNIT_WORDS : (s % 2 + 1) * 4 * UNIT_WORDS]
-            if (s, "done") in x_split:
-                flip(copy, x_split[s // 2][:, s % 2 * DM : (s % 2 + 1) * DM], grouped, True)
-            else:
-                flip(copy, raw_unit(s), grouped, False)
-
-        def quantise_x(s, n):
-            cols = slice(s * UNIT_WORDS, (s + n) * UNIT_WORDS)
-            grouped = x_grouped[s // 2][:, s % 2 * 4 * UNIT_WORDS : (s % 2 + n) * 4 * UNIT_WORDS]
-            quantise(grouped, val_codes[:, cols], val_scales[:, cols])
-
-        def logw_as_floats(i):
-            positions = slice(GROUP * i, GROUP * (i + 1))
-            S(out=lw[:, positions, :], in_=lw_bf[:, positions, :])
-
-        def split_wv(u, copy):
-            wv_split[u] = stage.tile([P, DM], BF16, tag="w_split", name="w_split")
-            split_words(copy, w_unit(wv_raw, u), wv_split[u][:])
-
-        def flip_wv(u, copy):
-            wv_grouped[u] = stage.tile([P, 4 * UNIT_WORDS], BF16, tag="w_grouped", bufs=6, align_bytes=64, name="w_grouped")
-            if u in wv_split:
-                flip(copy, wv_split[u][:], wv_grouped[u][:], True)
-            else:
-                flip(copy, w_unit(wv_raw, u), wv_grouped[u][:], False)
-
-        def split_wo(u, copy):
-            split_words(copy, w_unit(wo_raw, u), w_unit(wv_raw, u))
-            wo_grouped[u, "done"] = True
-
-        def flip_wo(u, copy):
-            done = (u, "done") in wo_grouped
-            wo_grouped[u] = stage.tile([P, 4 * UNIT_WORDS], BF16, tag="w_grouped", bufs=6, align_bytes=64, name="w_grouped")
-            flip(copy, w_unit(wv_raw if done else wo_raw, u), wo_grouped[u][:], done)
-
-        def quantise_w(grouped, codes, scales, u):
+        def quantise_weight(grouped, codes, scales, u):
             for g in range(PASSES):
                 cols = slice(g * DP + u * P, g * DP + (u + 1) * P)
                 quantise(grouped[:, g * 4 * P : (g + 1) * 4 * P], codes[:, cols], scales[:, cols])
 
+        wv_split, wv_grouped, wo_grouped, x_split, x_grouped, projected = {}, {}, {}, {}, {}, {}
+        split_positions = set()
+
+        def split_wv(u):
+            wv_split[u] = stage.tile([P, DM], BF16, tag="w_split", name="w_split")
+            split(on_vector, unit_of(wv_raw, u), wv_split[u][:])
+
+        def flip_wv(u):
+            wv_grouped[u] = stage.tile(
+                [P, UNIT_GROUPED], BF16, tag="w_grouped", name="w_grouped", bufs=6, align_bytes=64
+            )
+            flip(on_scalar, wv_split[u][:], wv_grouped[u][:], True)
+
         def quantise_wv(u):
-            quantise_w(wv_grouped[u], wv_codes, wv_scales, u)
+            quantise_weight(wv_grouped[u], wv_codes, wv_scales, u)
+
+        def split_wo(u):
+            split(on_scalar, unit_of(wo_raw, u), unit_of(wv_raw, u))
+
+        def flip_wo(u):
+            wo_grouped[u] = stage.tile(
+                [P, UNIT_GROUPED], BF16, tag="w_grouped", name="w_grouped", bufs=6, align_bytes=64
+            )
+            flip(on_scalar, unit_of(wv_raw, u), wo_grouped[u][:], True)
 
         def quantise_wo(u):
-            quantise_w(wo_grouped[u], wo_codes, wo_scales, u)
+            quantise_weight(wo_grouped[u], wo_codes, wo_scales, u)
+
+        def split_x(s, copy):
+            if s // 2 not in x_split:
+                x_split[s // 2] = stage.tile([P, 2 * DM], BF16, tag="x_split", name="x_split")
+            split(copy, unit_of(x_raw, s), unit_of(x_split[s // 2], s % 2))
+            split_positions.add(s)
+
+        def flip_x(s):
+            if s // 2 not in x_grouped:
+                x_grouped[s // 2] = stage.tile(
+                    [P, 2 * UNIT_GROUPED], BF16, tag="x_grouped", name="x_grouped", align_bytes=64
+                )
+            is_split = s in split_positions
+            rows = unit_of(x_split[s // 2], s % 2) if is_split else unit_of(x_raw, s)
+            grouped = x_grouped[s // 2][:, s % 2 * UNIT_GROUPED : (s % 2 + 1) * UNIT_GROUPED]
+            flip(on_scalar, rows, grouped, is_split)
+
+        def quantise_x(s, n):
+            cols = slice(s * UNIT_WORDS, (s + n) * UNIT_WORDS)
+            grouped = x_grouped[s // 2][:, s % 2 * UNIT_GROUPED : (s % 2 + n) * UNIT_GROUPED]
+            quantise(grouped, x_codes[:, cols], x_scales[:, cols])
+
+        def logw_for_side(i):
+            positions = slice(ROUND * i, ROUND * (i + 1))
+            nc.scalar.copy(out=logw_side[:, positions, :], in_=logw_raw[:, positions, :])
 
         def project(s, half):
-            vps[s, half] = banks.tile([P, N_TILE], F32, tag="bank", name="vp")
+            vp = banks.tile([P, N_TILE], F32, tag="bank")
+            projected[s, half] = vp
             for g in range(PASSES):
                 rows = slice((s * PASSES + g) * P, (s * PASSES + g + 1) * P)
                 cols = slice(g * DP + half * N_TILE, g * DP + (half + 1) * N_TILE)
                 nc.tensor.matmul_mx(
-                    out=vps[s, half][:],
-                    lhsT=val_codes[:, rows].bitcast(FP8X4),
-                    lhsT_scale=val_scales[:, rows],
+                    out=vp[:],
+                    lhsT=x_codes[:, rows].bitcast(FP8X4),
+                    lhsT_scale=x_scales[:, rows],
                     rhs=wv_codes[:, cols].bitcast(FP8X4),
                     rhs_scale=wv_scales[:, cols],
                     start=(g == 0),
                     stop=(g == PASSES - 1),
                 )
 
-        def pool(s, half, on_the_side=False):
-            vp = vps[s, half]
-            target = attn if (s, half) == (SL - 1, 1) else acc
-            if on_the_side:
-                weighted = stage.tile([P, N_TILE], F32, tag="weighted", bufs=3)
+        def pool(s, half):
+            total = attn if (s, half) == (SL - 1, 1) else acc
             for j in range(HEADS_PER_HALF):
                 h = half * HEADS_PER_HALF + j
                 channels = slice(h * HEAD_DIM, (h + 1) * HEAD_DIM)
-                bank_cols = slice(j * HEAD_DIM, (j + 1) * HEAD_DIM)
-                if on_the_side:
-                    nc.scalar.activation(
-                        out=weighted[:, bank_cols], in_=vp[:, bank_cols], func=COPY, scale=lw[:, s, h : h + 1]
-                    )
-                else:
-                    nc.vector.scalar_tensor_tensor(
-                        out=target[:, channels],
-                        in0=vp[:, bank_cols],
-                        scalar=lw_bf[:, s, h : h + 1],
-                        in1=acc[:, channels],
-                        op0=MULT,
-                        op1=ADD,
-                    )
-            if on_the_side:
-                side = acc_side[:, half * N_TILE : (half + 1) * N_TILE]
-                w = N_TILE // 1
-                for c in range(0, N_TILE, w):
-                    piece = slice(c, c + w)
-                    nc.gpsimd.tensor_tensor(out=side[:, piece], in0=side[:, piece], in1=weighted[:, piece], op=ADD)
+                nc.vector.scalar_tensor_tensor(
+                    out=total[:, channels],
+                    in0=projected[s, half][:, j * HEAD_DIM : (j + 1) * HEAD_DIM],
+                    scalar=logw_raw[:, s, h : h + 1],
+                    in1=acc[:, channels],
+                    op0=MULT,
+                    op1=ADD,
+                )
 
-        def join_sums(half, out):
-            cols = slice(half * N_TILE, (half + 1) * N_TILE)
-            nc.gpsimd.tensor_tensor(out=out[:, cols], in0=acc[:, cols], in1=acc_side[:, cols], op=ADD)
+        def pool_on_the_side(s):
+            weighted = stage.tile([P, N_TILE], F32, tag="weighted", bufs=3)
+            for h in range(HEADS_PER_HALF):
+                channels = slice(h * HEAD_DIM, (h + 1) * HEAD_DIM)
+                nc.scalar.activation(
+                    out=weighted[:, channels],
+                    in_=projected[s, 0][:, channels],
+                    func=COPY,
+                    scale=logw_side[:, s, h : h + 1],
+                )
+            nc.gpsimd.tensor_tensor(out=acc_side[:], in0=acc_side[:], in1=weighted[:], op=ADD)
+
+        def join_first_half():
+            first = slice(0, N_TILE)
+            nc.gpsimd.tensor_tensor(out=attn[:, first], in0=acc[:, first], in1=acc_side[:], op=ADD)
 
         def warm_up(n):
             for repeat in range(n):
@@ -267,20 +237,102 @@ def tile_multiheadattention_pb_kernel(tc, values, logw, Wv, Wo, out):
             flipped = banks.tile([P, 2, P], F32, tag="bank")
             for u in range(2):
                 nc.tensor.transpose(flipped[:, u, :], words[:, 2 * P * g + u : 2 * P * (g + 1) : 2], ident[:])
+            grouped = attn_grouped[:, g * 4 * P : (g + 1) * 4 * P]
             copy(
-                out=attn_grouped[:, g * 4 * P : (g + 1) * 4 * P].bitcast(F32).rearrange("p (b u) -> p b u", u=2),
+                out=grouped.bitcast(F32).rearrange("p (b u) -> p b u", u=2),
                 in_=flipped[:].rearrange("p u b -> p b u"),
             )
-
-        def quantise_attn(g):
             cols = slice(g * P, (g + 1) * P)
-            quantise(attn_grouped[:, g * 4 * P : (g + 1) * 4 * P], attn_codes[:, cols], attn_scales[:, cols])
+            quantise(grouped, attn_codes[:, cols], attn_scales[:, cols])
 
-        quarter = DO // 4
+        first_units = [(split_wv, flip_wv, quantise_wv, u) for u in range(4)]
+        first_units += [
+            (lambda s: split_x(s, on_vector), flip_x, lambda s: quantise_x(s, 1), s) for s in range(4)
+        ]
+        warm_up(5)
+        for n, (split_it, flip_it, quantise_it, u) in enumerate(first_units):
+            split_it(u)
+            if n > 0:
+                warm_up(1)
+            flip_it(u)
+            if n >= 3:
+                quantise_previous, previous = first_units[n - 3][2:]
+                quantise_previous(previous)
+        for n in range(3):
+            quantise_x(n + 1, 1)
+            split_wv(4 + n)
+        split_wv(7)
+        for s in range(2):
+            project(s, 0)
+        for s in range(4, 6):
+            split_x(s, on_scalar)
+        for u in range(4, 8):
+            flip_wv(u)
+        for s in range(2):
+            pool(s, 0)
+        for s in range(2, 4):
+            project(s, 0)
+        for s in range(2, 4):
+            quantise_wv(s + 2)
+            pool(s, 0)
+        for s in range(4, 8):
+            flip_x(s)
+        warm_up(1)
+        quantise_wv(6)
+        quantise_wv(7)
+        logw_for_side(1)
+        for s in range(8, 12):
+            split_x(s, on_vector)
+        for s in range(4):
+            project(s, 1)
+            if s in (1, 2):
+                quantise_x(2 * s + 2, 2)
+            pool(s, 1)
 
-        def project_out(g):
-            for n in range(4):
-                cols = slice(g * DO + n * quarter, g * DO + (n + 1) * quarter)
+        for i in range(1, N_ROUNDS):
+            last = i == N_ROUNDS - 1
+            positions = range(ROUND * i, ROUND * (i + 1))
+            next_positions = range(ROUND * (i + 1), min(ROUND * (i + 2), SL))
+            if last:
+                steps = [(s, half) for half in range(HALVES) for s in positions]
+            else:
+                steps = [(s, half) for s in positions for half in range(HALVES)]
+            for s in next_positions:
+                flip_x(s)
+            if i in (5, 6):
+                for u in range(4 * (i - 5), 4 * (i - 4)):
+                    quantise_wo(u)
+            for n, (s, half) in enumerate(steps):
+                if i in (1, 2, 3) and n in (5, 7):
+                    split_wo(2 * (i - 1) + n // 7)
+                if i in (4, 5) and n == 4:
+                    for u in range(4 * (i - 4), 4 * (i - 3)):
+                        flip_wo(u)
+                if i == 4 and n in (5, 7):
+                    split_wo(6 + n // 7)
+                if not last and n < 2:
+                    quantise_x(next_positions[2 * n], 2)
+                if not last and n == 1:
+                    logw_for_side(i + 1)
+                project(s, half)
+                side = {N_ROUNDS - 2: (0, 2, 4), N_ROUNDS - 1: (0,)}.get(i, (2,))
+                if n in side:
+                    pool_on_the_side(s)
+                else:
+                    pool(s, half)
+                if n == 1 and i + 2 < N_ROUNDS:
+                    for ahead in range(ROUND * (i + 2), ROUND * (i + 3) - 1):
+                        split_x(ahead, on_scalar)
+                if last and n == 4:
+                    join_first_half()
+
+        pieces = DO // OUT_TILE
+        out_sums = [banks.tile([P, OUT_TILE], F32, tag="bank", name="out_sums%d" % n) for n in range(pieces)]
+        flip_attn(0, on_scalar)
+        flip_attn(1, on_vector)
+        for g in range(PASSES):
+            for n in range(pieces):
+                cols = slice(g * DO + n * OUT_TILE, g * DO + (n + 1) * OUT_TILE)
                 nc.tensor.matmul_mx(
                     out=out_sums[n][:],
                     lhsT=attn_codes[:, g * P : (g + 1) * P].bitcast(FP8X4),
@@ -290,282 +342,8 @@ def tile_multiheadattention_pb_kernel(tc, values, logw, Wv, Wo, out):
                     start=(g == 0),
                     stop=(g == PASSES - 1),
                 )
-
-        warm_up(5)
-        split_wv(0, V)
-        flip_wv(0, S)
-        split_wv(1, V)
-        warm_up(1)
-        flip_wv(1, S)
-        split_wv(2, V)
-        warm_up(1)
-        quantise_wv(0)
-        flip_wv(2, S)
-        split_wv(3, V)
-        quantise_wv(1)
-        flip_wv(3, S)
-        warm_up(1)
-        split_x(0, V)
-        quantise_wv(2)
-        flip_x(0, S)
-        split_x(1, V)
-        warm_up(1)
-        flip_x(1, S)
-        split_x(2, V)
-        warm_up(1)
-        flip_x(2, S)
-        split_x(3, V)
-        quantise_wv(3)
-        flip_x(3, S)
-        quantise_x(0, 1)
-        split_wv(4, V)
-        quantise_x(1, 1)
-        split_wv(5, V)
-        project(0, 0)
-        project(1, 0)
-        quantise_x(2, 1)
-        split_wv(6, V)
-        quantise_x(3, 1)
-        split_wv(7, V)
-        split_x(4, S)
-        split_x(5, S)
-        flip_wv(4, S)
-        flip_wv(5, S)
-        flip_wv(6, S)
-        flip_wv(7, S)
-        pool(0, 0)
-        pool(1, 0)
-        project(2, 0)
-        project(3, 0)
-        quantise_wv(4)
-        pool(2, 0)
-        quantise_wv(5)
-        pool(3, 0)
-        flip_x(4, S)
-        flip_x(5, S)
-        flip_x(6, S)
-        flip_x(7, S)
-        warm_up(1)
-        quantise_wv(6)
-        quantise_wv(7)
-        logw_as_floats(1)
-        split_x(8, V)
-        split_x(9, V)
-        split_x(10, V)
-        split_x(11, V)
-        project(0, 1)
-        pool(0, 1)
-        project(1, 1)
-        quantise_x(4, 2)
-        pool(1, 1)
-        project(2, 1)
-        quantise_x(6, 2)
-        pool(2, 1)
-        project(3, 1)
-        pool(3, 1)
-        flip_x(8, S)
-        flip_x(9, S)
-        flip_x(10, S)
-        flip_x(11, S)
-        quantise_x(8, 2)
-        project(4, 0)
-        pool(4, 0)
-        quantise_x(10, 2)
-        logw_as_floats(2)
-        project(4, 1)
-        pool(4, 1)
-        split_x(12, S)
-        split_x(13, S)
-        split_x(14, S)
-        project(5, 0)
-        pool(5, 0, True)
-        project(5, 1)
-        pool(5, 1)
-        project(6, 0)
-        pool(6, 0)
-        split_wo(0, S)
-        project(6, 1)
-        pool(6, 1)
-        project(7, 0)
-        pool(7, 0)
-        split_wo(1, S)
-        project(7, 1)
-        pool(7, 1)
-        flip_x(12, S)
-        flip_x(13, S)
-        flip_x(14, S)
-        flip_x(15, S)
-        quantise_x(12, 2)
-        project(8, 0)
-        pool(8, 0)
-        quantise_x(14, 2)
-        logw_as_floats(3)
-        project(8, 1)
-        pool(8, 1)
-        split_x(16, S)
-        split_x(17, S)
-        split_x(18, S)
-        project(9, 0)
-        pool(9, 0, True)
-        project(9, 1)
-        pool(9, 1)
-        project(10, 0)
-        pool(10, 0)
-        split_wo(2, S)
-        project(10, 1)
-        pool(10, 1)
-        project(11, 0)
-        pool(11, 0)
-        split_wo(3, S)
-        project(11, 1)
-        pool(11, 1)
-        flip_x(16, S)
-        flip_x(17, S)
-        flip_x(18, S)
-        flip_x(19, S)
-        quantise_x(16, 2)
-        project(12, 0)
-        pool(12, 0)
-        quantise_x(18, 2)
-        logw_as_floats(4)
-        project(12, 1)
-        pool(12, 1)
-        split_x(20, S)
-        split_x(21, S)
-        split_x(22, S)
-        project(13, 0)
-        pool(13, 0, True)
-        project(13, 1)
-        pool(13, 1)
-        project(14, 0)
-        pool(14, 0)
-        split_wo(4, S)
-        project(14, 1)
-        pool(14, 1)
-        project(15, 0)
-        pool(15, 0)
-        split_wo(5, S)
-        project(15, 1)
-        pool(15, 1)
-        flip_x(20, S)
-        flip_x(21, S)
-        flip_x(22, S)
-        flip_x(23, S)
-        quantise_x(20, 2)
-        project(16, 0)
-        pool(16, 0)
-        quantise_x(22, 2)
-        logw_as_floats(5)
-        project(16, 1)
-        pool(16, 1)
-        split_x(24, S)
-        split_x(25, S)
-        split_x(26, S)
-        project(17, 0)
-        pool(17, 0, True)
-        project(17, 1)
-        pool(17, 1)
-        flip_wo(0, S)
-        flip_wo(1, S)
-        flip_wo(2, S)
-        flip_wo(3, S)
-        project(18, 0)
-        pool(18, 0)
-        split_wo(6, S)
-        project(18, 1)
-        pool(18, 1)
-        project(19, 0)
-        pool(19, 0)
-        split_wo(7, S)
-        project(19, 1)
-        pool(19, 1)
-        flip_x(24, S)
-        flip_x(25, S)
-        flip_x(26, S)
-        flip_x(27, S)
-        quantise_wo(0)
-        quantise_wo(1)
-        quantise_wo(2)
-        quantise_wo(3)
-        quantise_x(24, 2)
-        project(20, 0)
-        pool(20, 0)
-        quantise_x(26, 2)
-        logw_as_floats(6)
-        project(20, 1)
-        pool(20, 1)
-        split_x(28, S)
-        split_x(29, S)
-        split_x(30, S)
-        project(21, 0)
-        pool(21, 0, True)
-        project(21, 1)
-        pool(21, 1)
-        flip_wo(4, S)
-        flip_wo(5, S)
-        flip_wo(6, S)
-        flip_wo(7, S)
-        project(22, 0)
-        pool(22, 0)
-        project(22, 1)
-        pool(22, 1)
-        project(23, 0)
-        pool(23, 0)
-        project(23, 1)
-        pool(23, 1)
-        flip_x(28, S)
-        flip_x(29, S)
-        flip_x(30, S)
-        flip_x(31, S)
-        quantise_wo(4)
-        quantise_wo(5)
-        quantise_wo(6)
-        quantise_wo(7)
-        quantise_x(28, 2)
-        project(24, 0)
-        pool(24, 0, True)
-        quantise_x(30, 2)
-        logw_as_floats(7)
-        project(24, 1)
-        pool(24, 1)
-        project(25, 0)
-        pool(25, 0, True)
-        project(25, 1)
-        pool(25, 1)
-        project(26, 0)
-        pool(26, 0, True)
-        project(26, 1)
-        pool(26, 1)
-        project(27, 0)
-        pool(27, 0)
-        project(27, 1)
-        pool(27, 1)
-        project(28, 0)
-        pool(28, 0, True)
-        project(29, 0)
-        pool(29, 0)
-        project(30, 0)
-        pool(30, 0)
-        project(31, 0)
-        pool(31, 0)
-        project(28, 1)
-        pool(28, 1)
-        join_sums(0, attn)
-        project(29, 1)
-        pool(29, 1)
-        project(30, 1)
-        pool(30, 1)
-        project(31, 1)
-        pool(31, 1)
-        out_sums = [banks.tile([P, quarter], F32, tag="bank", name="out_sums%d" % n) for n in range(4)]
-        flip_attn(0, S)
-        quantise_attn(0)
-        flip_attn(1, V)
-        quantise_attn(1)
-        project_out(0)
-        project_out(1)
-
-        for n in range(4):
-            cols = slice(n * quarter, (n + 1) * quarter)
-            (S, V)[n % 2](out=out_sb[:, cols], in_=out_sums[n][:])
-            (nc.scalar, nc.sync)[n % 2].dma_start(out=out[:, cols], in_=out_sb[:, cols])
+        for n in range(pieces):
+            cols = slice(n * OUT_TILE, (n + 1) * OUT_TILE)
+            copy, queue = ((on_scalar, nc.scalar), (on_vector, nc.sync))[n % 2]
+            copy(out=out_sb[:, cols], in_=out_sums[n][:])
+            queue.dma_start(out=out[:, cols], in_=out_sb[:, cols])

from contextlib import ExitStack

import concourse.mybir as mybir
from concourse.masks import make_identity

F32 = mybir.dt.float32
BF16 = mybir.dt.bfloat16
U32 = mybir.dt.uint32
U8 = mybir.dt.uint8
FP8X4 = mybir.dt.float8_e4m3fn_x4
MULT = mybir.AluOpType.mult
ADD = mybir.AluOpType.add
COPY = mybir.ActivationFunctionType.Copy

P = 128
SL, DM, HEADS, HEAD_DIM, DO = 32, 1024, 16, 64, 1024
DP = HEADS * HEAD_DIM
K_PASS = 512
PASSES = DM // K_PASS
N_TILE = 512
HALVES = DP // N_TILE
HEADS_PER_HALF = N_TILE // HEAD_DIM
W_UNITS = DP // P
UNIT_WORDS = PASSES * P
UNIT_GROUPED = 4 * UNIT_WORDS
ROUND = 4
N_ROUNDS = SL // ROUND
OUT_TILE = 256

FLOPS = 2 * SL * P * DM * DP + 2 * P * DP * DO


def tile_multiheadattention_pb_kernel(tc, values, logw, Wv, Wo, out):
    nc = tc.nc
    with ExitStack() as ctx:
        keep = ctx.enter_context(tc.tile_pool(name="keep", bufs=1))
        stage = ctx.enter_context(tc.tile_pool(name="stage", bufs=4))
        banks = ctx.enter_context(tc.psum_pool(name="banks", bufs=8))
        ctx.enter_context(tc.manual_schedule())

        ident = keep.tile([P, P], F32)
        make_identity(nc, ident[:])
        zeros = keep.tile([P, N_TILE], BF16)
        nc.vector.memset(zeros[:], 0.0)
        acc = keep.tile([P, DP], F32)
        nc.vector.memset(acc[:], 0.0)
        acc_side = keep.tile([P, N_TILE], F32)
        nc.gpsimd.memset(acc_side[:], 0.0)

        x_raw = keep.tile([P, SL * DM], BF16)
        wv_raw = keep.tile([P, W_UNITS * DM], BF16)
        wo_raw = keep.tile([P, W_UNITS * DM], BF16)
        logw_raw = keep.tile([P, SL, HEADS], BF16)
        logw_side = keep.tile([P, SL, HEADS], F32)
        x_codes = keep.tile([P, SL * UNIT_WORDS], U32, align_bytes=64)
        x_scales = keep.tile([P, SL * UNIT_WORDS], U8, align_bytes=64)
        wv_codes = keep.tile([P, PASSES * DP], U32, align_bytes=64)
        wv_scales = keep.tile([P, PASSES * DP], U8, align_bytes=64)
        wo_codes = keep.tile([P, PASSES * DO], U32, align_bytes=64)
        wo_scales = keep.tile([P, PASSES * DO], U8, align_bytes=64)
        attn = keep.tile([P, DP], BF16)
        attn_grouped = keep.tile([P, UNIT_GROUPED], BF16, align_bytes=64)
        attn_codes = keep.tile([P, UNIT_WORDS], U32, align_bytes=64)
        attn_scales = keep.tile([P, UNIT_WORDS], U8, align_bytes=64)
        out_sb = keep.tile([P, DO], F32)

        def load(raw, matrix, unit, n):
            src = matrix[unit * P : (unit + n) * P, :].rearrange("(t p) k -> p t k", p=P)
            dst = raw[:, unit * DM : (unit + n) * DM].rearrange("p (t k) -> p t k", t=n)
            nc.sync.dma_start(out=dst, in_=src)

        value_rows = values.flatten_outer_dims()

        def load_logw(i):
            positions = slice(ROUND * i, ROUND * (i + 1))
            nc.sync.dma_start(
                out=logw_raw[:, positions, :], in_=logw[positions].rearrange("s b h -> b s h")
            )

        for u in range(4):
            load(wv_raw, Wv, u, 1)
        for s in range(4):
            load(x_raw, value_rows, s, 1)
        for u in range(4, 8):
            load(wv_raw, Wv, u, 1)
        load_logw(0)
        for s in range(4, 8):
            load(x_raw, value_rows, s, 1)
        load_logw(1)
        for i in range(2, N_ROUNDS):
            load(x_raw, value_rows, ROUND * i, 2)
            load(x_raw, value_rows, ROUND * i + 2, 2)
            load_logw(i)
            if i in (2, 3, 4, 5):
                load(wo_raw, Wo, 2 * (i - 2), 2)

        on_vector, on_scalar = nc.vector.tensor_copy, nc.scalar.copy

        def unit_of(tile, u):
            return tile[:, u * DM : (u + 1) * DM]

        def split(copy, raw, halves):
            copy(
                out=halves.bitcast(F32).rearrange("p (u w) -> p u w", u=2),
                in_=raw.bitcast(F32).rearrange("p (w u) -> p u w", u=2),
            )

        def flip(copy, rows, grouped, is_split):
            words = rows.bitcast(F32)
            flipped = banks.tile([P, PASSES, 2, P], F32, tag="bank")
            for g in range(PASSES):
                for u in range(2):
                    if is_split:
                        these = words[:, u * UNIT_WORDS + g * P : u * UNIT_WORDS + (g + 1) * P]
                    else:
                        these = words[:, 2 * P * g + u : 2 * P * (g + 1) : 2]
                    nc.tensor.transpose(flipped[:, g, u, :], these, ident[:])
            copy(
                out=grouped.bitcast(F32).rearrange("p (g r u) -> p g r u", g=PASSES, u=2),
                in_=flipped[:].rearrange("p g u r -> p g r u"),
            )

        def quantise(grouped, codes, scales):
            nc.vector.quantize_mx(out=codes.bitcast(FP8X4), scales=scales, in_=grouped)

        def quantise_weight(grouped, codes, scales, u):
            for g in range(PASSES):
                cols = slice(g * DP + u * P, g * DP + (u + 1) * P)
                quantise(grouped[:, g * 4 * P : (g + 1) * 4 * P], codes[:, cols], scales[:, cols])

        wv_split, wv_grouped, wo_grouped, x_split, x_grouped, projected = {}, {}, {}, {}, {}, {}
        split_positions = set()

        def split_wv(u):
            wv_split[u] = stage.tile([P, DM], BF16, tag="w_split", name="w_split")
            split(on_vector, unit_of(wv_raw, u), wv_split[u][:])

        def flip_wv(u):
            wv_grouped[u] = stage.tile(
                [P, UNIT_GROUPED], BF16, tag="w_grouped", name="w_grouped", bufs=6, align_bytes=64
            )
            flip(on_scalar, wv_split[u][:], wv_grouped[u][:], True)

        def quantise_wv(u):
            quantise_weight(wv_grouped[u], wv_codes, wv_scales, u)

        def split_wo(u):
            split(on_scalar, unit_of(wo_raw, u), unit_of(wv_raw, u))

        def flip_wo(u):
            wo_grouped[u] = stage.tile(
                [P, UNIT_GROUPED], BF16, tag="w_grouped", name="w_grouped", bufs=6, align_bytes=64
            )
            flip(on_scalar, unit_of(wv_raw, u), wo_grouped[u][:], True)

        def quantise_wo(u):
            quantise_weight(wo_grouped[u], wo_codes, wo_scales, u)

        def split_x(s, copy):
            if s // 2 not in x_split:
                x_split[s // 2] = stage.tile([P, 2 * DM], BF16, tag="x_split", name="x_split")
            split(copy, unit_of(x_raw, s), unit_of(x_split[s // 2], s % 2))
            split_positions.add(s)

        def flip_x(s):
            if s // 2 not in x_grouped:
                x_grouped[s // 2] = stage.tile(
                    [P, 2 * UNIT_GROUPED], BF16, tag="x_grouped", name="x_grouped", align_bytes=64
                )
            is_split = s in split_positions
            rows = unit_of(x_split[s // 2], s % 2) if is_split else unit_of(x_raw, s)
            grouped = x_grouped[s // 2][:, s % 2 * UNIT_GROUPED : (s % 2 + 1) * UNIT_GROUPED]
            flip(on_scalar, rows, grouped, is_split)

        def quantise_x(s, n):
            cols = slice(s * UNIT_WORDS, (s + n) * UNIT_WORDS)
            grouped = x_grouped[s // 2][:, s % 2 * UNIT_GROUPED : (s % 2 + n) * UNIT_GROUPED]
            quantise(grouped, x_codes[:, cols], x_scales[:, cols])

        def logw_for_side(i):
            positions = slice(ROUND * i, ROUND * (i + 1))
            nc.scalar.copy(out=logw_side[:, positions, :], in_=logw_raw[:, positions, :])

        def project(s, half):
            vp = banks.tile([P, N_TILE], F32, tag="bank")
            projected[s, half] = vp
            for g in range(PASSES):
                rows = slice((s * PASSES + g) * P, (s * PASSES + g + 1) * P)
                cols = slice(g * DP + half * N_TILE, g * DP + (half + 1) * N_TILE)
                nc.tensor.matmul_mx(
                    out=vp[:],
                    lhsT=x_codes[:, rows].bitcast(FP8X4),
                    lhsT_scale=x_scales[:, rows],
                    rhs=wv_codes[:, cols].bitcast(FP8X4),
                    rhs_scale=wv_scales[:, cols],
                    start=(g == 0),
                    stop=(g == PASSES - 1),
                )

        def pool(s, half):
            total = attn if (s, half) == (SL - 1, 1) else acc
            for j in range(HEADS_PER_HALF):
                h = half * HEADS_PER_HALF + j
                channels = slice(h * HEAD_DIM, (h + 1) * HEAD_DIM)
                nc.vector.scalar_tensor_tensor(
                    out=total[:, channels],
                    in0=projected[s, half][:, j * HEAD_DIM : (j + 1) * HEAD_DIM],
                    scalar=logw_raw[:, s, h : h + 1],
                    in1=acc[:, channels],
                    op0=MULT,
                    op1=ADD,
                )

        def pool_on_the_side(s):
            weighted = stage.tile([P, N_TILE], F32, tag="weighted", bufs=3)
            for h in range(HEADS_PER_HALF):
                channels = slice(h * HEAD_DIM, (h + 1) * HEAD_DIM)
                nc.scalar.activation(
                    out=weighted[:, channels],
                    in_=projected[s, 0][:, channels],
                    func=COPY,
                    scale=logw_side[:, s, h : h + 1],
                )
            nc.gpsimd.tensor_tensor(out=acc_side[:], in0=acc_side[:], in1=weighted[:], op=ADD)

        def join_first_half():
            first = slice(0, N_TILE)
            nc.gpsimd.tensor_tensor(out=attn[:, first], in0=acc[:, first], in1=acc_side[:], op=ADD)

        def warm_up(n):
            for repeat in range(n):
                scratch = banks.tile([P, N_TILE], F32, tag="bank")
                nc.tensor.matmul(out=scratch[:], lhsT=zeros[:, 0:P], rhs=zeros[:], start=True, stop=True)

        def flip_attn(g, copy):
            words = attn[:].bitcast(F32)
            flipped = banks.tile([P, 2, P], F32, tag="bank")
            for u in range(2):
                nc.tensor.transpose(flipped[:, u, :], words[:, 2 * P * g + u : 2 * P * (g + 1) : 2], ident[:])
            grouped = attn_grouped[:, g * 4 * P : (g + 1) * 4 * P]
            copy(
                out=grouped.bitcast(F32).rearrange("p (b u) -> p b u", u=2),
                in_=flipped[:].rearrange("p u b -> p b u"),
            )
            cols = slice(g * P, (g + 1) * P)
            quantise(grouped, attn_codes[:, cols], attn_scales[:, cols])

        first_units = [(split_wv, flip_wv, quantise_wv, u) for u in range(4)]
        first_units += [
            (lambda s: split_x(s, on_vector), flip_x, lambda s: quantise_x(s, 1), s) for s in range(4)
        ]
        warm_up(5)
        for n, (split_it, flip_it, quantise_it, u) in enumerate(first_units):
            split_it(u)
            if n > 0:
                warm_up(1)
            flip_it(u)
            if n >= 3:
                quantise_previous, previous = first_units[n - 3][2:]
                quantise_previous(previous)
        for n in range(3):
            quantise_x(n + 1, 1)
            split_wv(4 + n)
        split_wv(7)
        for s in range(2):
            project(s, 0)
        for s in range(4, 6):
            split_x(s, on_scalar)
        for u in range(4, 8):
            flip_wv(u)
        for s in range(2):
            pool(s, 0)
        for s in range(2, 4):
            project(s, 0)
        for s in range(2, 4):
            quantise_wv(s + 2)
            pool(s, 0)
        for s in range(4, 8):
            flip_x(s)
        warm_up(1)
        quantise_wv(6)
        quantise_wv(7)
        logw_for_side(1)
        for s in range(8, 12):
            split_x(s, on_vector)
        for s in range(4):
            project(s, 1)
            if s in (1, 2):
                quantise_x(2 * s + 2, 2)
            pool(s, 1)

        for i in range(1, N_ROUNDS):
            last = i == N_ROUNDS - 1
            positions = range(ROUND * i, ROUND * (i + 1))
            next_positions = range(ROUND * (i + 1), min(ROUND * (i + 2), SL))
            if last:
                steps = [(s, half) for half in range(HALVES) for s in positions]
            else:
                steps = [(s, half) for s in positions for half in range(HALVES)]
            for s in next_positions:
                flip_x(s)
            if i in (5, 6):
                for u in range(4 * (i - 5), 4 * (i - 4)):
                    quantise_wo(u)
            for n, (s, half) in enumerate(steps):
                if i in (1, 2, 3) and n in (5, 7):
                    split_wo(2 * (i - 1) + n // 7)
                if i in (4, 5) and n == 4:
                    for u in range(4 * (i - 4), 4 * (i - 3)):
                        flip_wo(u)
                if i == 4 and n in (5, 7):
                    split_wo(6 + n // 7)
                if not last and n < 2:
                    quantise_x(next_positions[2 * n], 2)
                if not last and n == 1:
                    logw_for_side(i + 1)
                project(s, half)
                side = {N_ROUNDS - 2: (0, 2, 4), N_ROUNDS - 1: (0,)}.get(i, (2,))
                if n in side:
                    pool_on_the_side(s)
                else:
                    pool(s, half)
                if n == 1 and i + 2 < N_ROUNDS:
                    for ahead in range(ROUND * (i + 2), ROUND * (i + 3) - 1):
                        split_x(ahead, on_scalar)
                if last and n == 4:
                    join_first_half()

        pieces = DO // OUT_TILE
        out_sums = [banks.tile([P, OUT_TILE], F32, tag="bank", name="out_sums%d" % n) for n in range(pieces)]
        flip_attn(0, on_scalar)
        flip_attn(1, on_vector)
        for g in range(PASSES):
            for n in range(pieces):
                cols = slice(g * DO + n * OUT_TILE, g * DO + (n + 1) * OUT_TILE)
                nc.tensor.matmul_mx(
                    out=out_sums[n][:],
                    lhsT=attn_codes[:, g * P : (g + 1) * P].bitcast(FP8X4),
                    lhsT_scale=attn_scales[:, g * P : (g + 1) * P],
                    rhs=wo_codes[:, cols].bitcast(FP8X4),
                    rhs_scale=wo_scales[:, cols],
                    start=(g == 0),
                    stop=(g == PASSES - 1),
                )
        for n in range(pieces):
            cols = slice(n * OUT_TILE, (n + 1) * OUT_TILE)
            copy, queue = ((on_scalar, nc.scalar), (on_vector, nc.sync))[n % 2]
            copy(out=out_sb[:, cols], in_=out_sums[n][:])
            queue.dma_start(out=out[:, cols], in_=out_sb[:, cols])
